import numpy as np
import ml_dtypes


def mxq(x, axis, fmt="e4m3"):
    dtype, down = {"e4m3": (ml_dtypes.float8_e4m3fn, 7), "e5m2": (ml_dtypes.float8_e5m2, 14)}[fmt]
    v = np.moveaxis(np.asarray(x, np.float32).astype(ml_dtypes.bfloat16).astype(np.float64), axis, -1)
    blocks = v.reshape(v.shape[:-1] + (-1, 32))
    amax = np.abs(blocks).max(-1, keepdims=True)
    byte = np.maximum(np.where(amax > 0, np.frexp(amax)[1] - 1 + 127, 0) - down, 1)
    scale = np.exp2(byte - 127.0)
    codes = (blocks / scale).astype(np.float32).astype(dtype).astype(np.float64)
    return np.moveaxis((codes * scale).reshape(v.shape), -1, axis)


WIDE = False


def mx_kscale(k):
    if not WIDE:
        return np.ones(k)
    levels = np.array([10, -10, 5, -5, 0])
    a = np.random.permutation(np.resize(levels, k // 512 * 4)).reshape(k // 512, 4)
    idx = np.arange(k)
    return np.exp2(a[idx // 512, idx % 128 // 32])


BF16 = ml_dtypes.bfloat16


def bf(x):
    return np.asarray(x, np.float32).astype(BF16)


def f64(x):
    return np.asarray(x).astype(np.float64)


B, D_IN, HID, F = 512, 2048, 2048, 512
L = 2 * F


def koopman_rotate(enc_x, delta_t, amplitudes, frequencies):
    n = enc_x.shape[0]
    amp = amplitudes[None, :] ** delta_t[:, None]
    ang = frequencies[None, :] * delta_t[:, None]
    c = amp * np.cos(ang)
    sn = amp * np.sin(ang)
    xe = enc_x.reshape(n, -1, 2)
    ev, od = xe[..., 0], xe[..., 1]
    out = np.stack([c * ev - sn * od, sn * ev + c * od], axis=-1)
    return out.reshape(n, -1)


def setup_inputs():
    s = mx_kscale(D_IN)
    return {
        "x": bf(np.random.standard_normal((B, D_IN)) * s),
        "delta_t": bf(np.random.uniform(0.1, 1.0, B)),
        "W_enc1": bf(np.random.standard_normal((D_IN, HID)) / np.sqrt(D_IN) / s[:, None]),
        "b_enc1": bf(np.random.standard_normal(HID) * 0.2),
        "W_enc2": bf(np.random.standard_normal((HID, L)) / np.sqrt(HID)),
        "b_enc2": bf(np.random.standard_normal(L) * 0.2),
        "amplitudes": bf(np.random.uniform(0.5, 1.5, F)),
        "frequencies": bf(np.random.uniform(0.0, 2.0 * np.pi, F)),
    }


def reference(x, delta_t, W_enc1, b_enc1, W_enc2, b_enc2, amplitudes, frequencies):
    h = np.tanh((mxq(f64(x), 1, "e4m3") @ mxq(f64(W_enc1), 0, "e4m3")) + f64(b_enc1))
    enc_x = (mxq(h, 1, "e4m3") @ mxq(f64(W_enc2), 0, "e4m3")) + f64(b_enc2)
    enc_pred = koopman_rotate(enc_x, f64(delta_t), f64(amplitudes), f64(frequencies))
    return (enc_pred, enc_x)

@@ -1,0 +1,401 @@
+import math
+from contextlib import ExitStack
+
+import concourse.mybir as mybir
+from concourse.masks import make_identity
+
+F32 = mybir.dt.float32
+BF16 = mybir.dt.bfloat16
+U32 = mybir.dt.uint32
+U8 = mybir.dt.uint8
+FP8X4 = mybir.dt.float8_e4m3fn_x4
+ALU = mybir.AluOpType
+ACT = mybir.ActivationFunctionType
+
+P = 128
+PACK = 4
+K_PASS = P * PACK
+
+BATCH, D_IN, HID, PAIRS = 512, 2048, 2048, 512
+LATENT = 2 * PAIRS
+BATCH_TILES = BATCH // P
+PASSES = D_IN // K_PASS
+HID_TILES = HID // P
+
+W1_CHUNK = K_PASS
+W1_CHUNKS = HID // W1_CHUNK
+W2_CHUNK = 256
+W2_CHUNKS = LATENT // W2_CHUNK
+CHUNK_PAIRS = W2_CHUNK // 2
+
+W1_VECTOR_COLS = 288
+SCALAR_LEAD = 3
+W1_RAW_BUFS = 6
+
+ROUND_TO_WHOLE = 1.5 * 2.0**23
+
+FLOPS = 2 * BATCH * D_IN * HID + 2 * BATCH * HID * LATENT
+
+
+def regroup(copy, grouped, planes):
+    copy(
+        out=grouped.rearrange("p (c i) t -> p c t i", i=4),
+        in_=planes.rearrange("p t (c i) -> p c t i", i=4),
+    )
+
+
+def tile_koopmanae_pa_kernel(
+    tc, x, delta_t, W_enc1, b_enc1, W_enc2, b_enc2, amplitudes, frequencies, out_0, out_1
+):
+    nc = tc.nc
+    with ExitStack() as ctx:
+        ctx.enter_context(tc.manual_schedule())
+        keep = ctx.enter_context(tc.tile_pool(name="keep", bufs=1))
+        w1_raw_pool = ctx.enter_context(tc.tile_pool(name="w1_raw", bufs=W1_RAW_BUFS))
+        w1_grouped_pool = ctx.enter_context(tc.tile_pool(name="w1_grouped", bufs=SCALAR_LEAD + 2))
+        grouped_pool = ctx.enter_context(tc.tile_pool(name="grouped", bufs=3))
+        w1_mx_pool = ctx.enter_context(tc.tile_pool(name="w1_mx", bufs=2))
+        psum_h = ctx.enter_context(tc.psum_pool(name="psum_h", bufs=6))
+        psum_small = ctx.enter_context(tc.psum_pool(name="psum_small", bufs=2))
+
+        x_codes = keep.tile([P, PASSES, BATCH], U32, align_bytes=64)
+        x_scales = keep.tile([P, PASSES, BATCH], U8, align_bytes=64)
+        h_codes = keep.tile([P, PASSES, BATCH], U32, align_bytes=64)
+        h_scales = keep.tile([P, PASSES, BATCH], U8, align_bytes=64)
+        w2_codes = keep.tile([P, W2_CHUNKS, PASSES, W2_CHUNK], U32, align_bytes=64)
+        w2_scales = keep.tile([P, W2_CHUNKS, PASSES, W2_CHUNK], U8, align_bytes=64)
+
+        ident_bf16 = keep.tile([P, P], BF16)
+        make_identity(nc, ident_bf16[:])
+        ident_f32 = keep.tile([P, P], F32)
+        make_identity(nc, ident_f32[:])
+
+        rows = keep.tile([P, P], BF16)
+        nc.vector.memset(rows[:], 0.0)
+        nc.sync.dma_start(out=rows[0:HID_TILES, :], in_=b_enc1.rearrange("(m p) -> m p", p=P))
+        nc.sync.dma_start(
+            out=rows[HID_TILES : HID_TILES + BATCH_TILES, :],
+            in_=delta_t.rearrange("(b p) -> b p", p=P),
+        )
+
+        w1_rows = W_enc1.rearrange("(g p j) n -> g p j n", p=P, j=PACK)
+        w2_rows = W_enc2.rearrange("(g t p) n -> g p t n", t=PACK, p=P)
+        w2_raw = keep.tile([P, PASSES, PACK, LATENT], BF16)
+        n_pieces = W1_CHUNKS * PASSES
+        w1_raw = {}
+
+        def load_w1_piece(k):
+            c, g = divmod(k, PASSES)
+            w1_raw[k] = w1_raw_pool.tile([P, PACK, W1_CHUNK], BF16, name="w1_raw")
+            nc.sync.dma_start(
+                out=w1_raw[k][:], in_=w1_rows[g, :, :, c * W1_CHUNK : (c + 1) * W1_CHUNK]
+            )
+            if g == PASSES - 1:
+                nc.sync.dma_start(out=w2_raw[:, c, :, :], in_=w2_rows[c])
+
+        with tc.tile_pool(name="early", bufs=1) as early, tc.tile_pool(name="turns", bufs=2) as turns:
+            x_sb = early.tile([P, BATCH_TILES, D_IN], BF16)
+            for b in range(BATCH_TILES):
+                nc.sync.dma_start(out=x_sb[:, b, :], in_=x[b * P : (b + 1) * P, :])
+            for k in range(W1_RAW_BUFS):
+                load_w1_piece(k)
+            freq_all = early.tile([P, PAIRS], BF16)
+            nc.scalar.dma_start(out=freq_all[:], in_=frequencies.partition_broadcast(P))
+            ampl_all = early.tile([P, PAIRS], BF16)
+            nc.scalar.dma_start(out=ampl_all[:], in_=amplitudes.partition_broadcast(P))
+
+            columns_ps = psum_small.tile([P, P], BF16, tag="small")
+            nc.tensor.transpose(columns_ps[:], rows[:], ident_bf16[:])
+            columns = keep.tile([P, HID_TILES + BATCH_TILES], F32)
+            nc.vector.tensor_copy(out=columns[:], in_=columns_ps[:, 0 : HID_TILES + BATCH_TILES])
+            b1_col = columns[:, 0:HID_TILES]
+            dt_col = columns[:, HID_TILES : HID_TILES + BATCH_TILES]
+
+            ln_ampl = early.tile([P, PAIRS], F32)
+            nc.scalar.activation(out=ln_ampl[:], in_=ampl_all[:], func=ACT.Ln)
+            power = keep.tile([P, BATCH_TILES, PAIRS], F32)
+            for b in range(BATCH_TILES):
+                nc.scalar.activation(
+                    out=power[:, b, :], in_=ln_ampl[:], func=ACT.Exp, scale=dt_col[:, b : b + 1]
+                )
+
+            dt_turns = keep.tile([P, BATCH_TILES], F32)
+            nc.vector.tensor_scalar(
+                out=dt_turns[:], in0=dt_col, scalar1=1.0 / (2.0 * math.pi), scalar2=None, op0=ALU.mult
+            )
+            part = early.tile([P, BATCH_TILES, PAIRS], F32)
+            for b in range(BATCH_TILES):
+                shifted = turns.tile([P, PAIRS], F32)
+                nc.vector.tensor_scalar(
+                    out=shifted[:],
+                    in0=freq_all[:],
+                    scalar1=dt_turns[:, b : b + 1],
+                    scalar2=ROUND_TO_WHOLE,
+                    op0=ALU.mult,
+                    op1=ALU.add,
+                )
+                whole = turns.tile([P, PAIRS], F32)
+                nc.vector.tensor_scalar(
+                    out=whole[:], in0=shifted[:], scalar1=ROUND_TO_WHOLE, scalar2=None, op0=ALU.subtract
+                )
+                nc.vector.scalar_tensor_tensor(
+                    out=part[:, b, :],
+                    in0=freq_all[:],
+                    scalar=dt_turns[:, b : b + 1],
+                    in1=whole[:],
+                    op0=ALU.mult,
+                    op1=ALU.subtract,
+                )
+            minus_abs_part = early.tile([P, BATCH_TILES, PAIRS], F32)
+            nc.vector.scalar_tensor_tensor(
+                out=minus_abs_part[:], in0=part[:], scalar=-1.0, in1=part[:], op0=ALU.mult, op1=ALU.min
+            )
+            sin_amp = keep.tile([P, BATCH_TILES, PAIRS], F32)
+            nc.scalar.activation(out=sin_amp[:], in_=part[:], func=ACT.Sin, scale=2.0 * math.pi)
+            cos_amp = keep.tile([P, BATCH_TILES, PAIRS], F32)
+            nc.scalar.activation(
+                out=cos_amp[:],
+                in_=minus_abs_part[:],
+                func=ACT.Sin,
+                scale=2.0 * math.pi,
+                bias=math.pi / 2.0,
+            )
+
+            x_grouped = {}
+
+            def quantise_x(g):
+                nc.vector.quantize_mx(
+                    out=x_codes[:, g, :].bitcast(FP8X4),
+                    scales=x_scales[:, g, :],
+                    in_=x_grouped[g][:].rearrange("p b t -> p (b t)"),
+                )
+
+            for g in range(PASSES):
+                x_grouped[g] = grouped_pool.tile(
+                    [P, BATCH, PACK], BF16, align_bytes=64, name="x_grouped", tag="grouped"
+                )
+                x_grouped_words = (
+                    x_grouped[g][:]
+                    .rearrange("p b t -> p (b t)")
+                    .bitcast(F32)
+                    .rearrange("p (b u) -> p b u", u=2)
+                )
+                for half in range(2):
+                    xt = psum_small.tile([P, 2, 2 * P], F32, tag="small")
+                    for j in range(2):
+                        words = (
+                            x_sb[:, 2 * half + j, :]
+                            .bitcast(F32)
+                            .rearrange("p (g q u) -> p g u q", g=PASSES, u=2)
+                        )
+                        for u in range(2):
+                            nc.tensor.transpose(
+                                xt[:, u, j * P : (j + 1) * P], words[:, g, u, :], ident_f32[:]
+                            )
+                    nc.vector.tensor_copy(
+                        out=x_grouped_words[:, half * 2 * P : (half + 1) * 2 * P, :],
+                        in_=xt[:].rearrange("p u b -> p b u"),
+                    )
+                if g > 0:
+                    quantise_x(g - 1)
+            quantise_x(PASSES - 1)
+
+        h_pool = ctx.enter_context(tc.tile_pool(name="h", bufs=2))
+        out_pool = ctx.enter_context(tc.tile_pool(name="out", bufs=2))
+        product_pool = ctx.enter_context(tc.tile_pool(name="product", bufs=1))
+
+        w1_grouped = {}
+        w1_mx = {}
+        h_acc = {}
+        h_planes = {}
+        h_grouped = {}
+        vector_cols = slice(0, W1_VECTOR_COLS)
+        scalar_cols = slice(W1_VECTOR_COLS, W1_CHUNK)
+
+        def scalar_regroups_w1(k):
+            w1_grouped[k] = w1_grouped_pool.tile(
+                [P, W1_CHUNK, PACK], BF16, align_bytes=64, name="w1_grouped"
+            )
+            regroup(nc.scalar.copy, w1_grouped[k][:, scalar_cols, :], w1_raw[k][:, :, scalar_cols])
+
+        def vector_regroups_w1(k):
+            regroup(nc.vector.tensor_copy, w1_grouped[k][:, vector_cols, :], w1_raw[k][:, :, vector_cols])
+
+        def multiply_w1_piece(k):
+            c, g = divmod(k, PASSES)
+            if g == 0:
+                w1_mx[c] = (
+                    w1_mx_pool.tile([P, PASSES, W1_CHUNK], U32, align_bytes=64, name="w1_codes"),
+                    w1_mx_pool.tile([P, PASSES, W1_CHUNK], U8, align_bytes=64, name="w1_scales"),
+                )
+                h_acc[c] = [psum_h.tile([P, BATCH], F32, name="h_acc") for t in range(PACK)]
+            codes, scales = w1_mx[c]
+            nc.vector.quantize_mx(
+                out=codes[:, g, :].bitcast(FP8X4),
+                scales=scales[:, g, :],
+                in_=w1_grouped[k][:].rearrange("p n t -> p (n t)"),
+            )
+            for t in range(PACK):
+                units = slice(t * P, (t + 1) * P)
+                nc.tensor.matmul_mx(
+                    out=h_acc[c][t][:],
+                    lhsT=codes[:, g, units].bitcast(FP8X4),
+                    lhsT_scale=scales[:, g, units],
+                    rhs=x_codes[:, g, :].bitcast(FP8X4),
+                    rhs_scale=x_scales[:, g, :],
+                    start=(g == 0),
+                    stop=(g == PASSES - 1),
+                )
+
+        def tanh_h(c):
+            h_planes[c] = h_pool.tile([P, PACK, BATCH], BF16, name="h_planes")
+            for t in range(PACK):
+                m = c * PACK + t
+                nc.scalar.activation(
+                    out=h_planes[c][:, t, :], in_=h_acc[c][t][:], func=ACT.Tanh, bias=b1_col[:, m : m + 1]
+                )
+
+        def regroup_h(c):
+            h_grouped[c] = grouped_pool.tile(
+                [P, BATCH, PACK], BF16, align_bytes=64, name="h_grouped", tag="grouped"
+            )
+            regroup(nc.vector.tensor_copy, h_grouped[c][:], h_planes[c][:])
+
+        def quantise_h(c):
+            nc.vector.quantize_mx(
+                out=h_codes[:, c, :].bitcast(FP8X4),
+                scales=h_scales[:, c, :],
+                in_=h_grouped[c][:].rearrange("p b t -> p (b t)"),
+            )
+
+        w2_grouped = {}
+        enc_acc = {}
+        enc = {}
+        enc_x_rows = out_1.rearrange("(b p) n -> p b n", p=P)
+        enc_pred_rows = out_0.rearrange("(b p) n -> p b n", p=P)
+
+        def scalar_regroups_w2(job):
+            c, g = divmod(job, PASSES)
+            if g % 2 == 0:
+                w2_grouped[(c, g)] = grouped_pool.tile(
+                    [P, 2, W2_CHUNK, PACK], BF16, align_bytes=64, name="w2_grouped", tag="grouped"
+                )
+            regroup(
+                nc.scalar.copy,
+                w2_grouped[(c, g - g % 2)][:, g % 2, :, :],
+                w2_raw[:, g, :, c * W2_CHUNK : (c + 1) * W2_CHUNK],
+            )
+
+        def quantise_w2(c, first):
+            nc.vector.quantize_mx(
+                out=w2_codes[:, c, first : first + 2, :].rearrange("p g n -> p (g n)").bitcast(FP8X4),
+                scales=w2_scales[:, c, first : first + 2, :].rearrange("p g n -> p (g n)"),
+                in_=w2_grouped[(c, first)][:].rearrange("p g n t -> p (g n t)"),
+            )
+
+        def multiply_w2_chunk(c):
+            for half in range(2):
+                enc_acc[(c, half)] = psum_small.tile([P, 2, W2_CHUNK], F32, name="enc_acc", tag="small")
+                for j in range(2):
+                    batch = slice((2 * half + j) * P, (2 * half + j + 1) * P)
+                    for g in range(PASSES):
+                        nc.tensor.matmul_mx(
+                            out=enc_acc[(c, half)][:, j, :],
+                            lhsT=h_codes[:, g, batch].bitcast(FP8X4),
+                            lhsT_scale=h_scales[:, g, batch],
+                            rhs=w2_codes[:, c, g, :].bitcast(FP8X4),
+                            rhs_scale=w2_scales[:, c, g, :],
+                            start=(g == 0),
+                            stop=(g == PASSES - 1),
+                        )
+
+        def add_b2(c):
+            cols = slice(c * W2_CHUNK, (c + 1) * W2_CHUNK)
+            enc[c] = out_pool.tile([P, BATCH_TILES, W2_CHUNK], F32, name="enc")
+            for half in range(2):
+                nc.vector.tensor_tensor(
+                    out=enc[c][:, 2 * half : 2 * half + 2, :],
+                    in0=enc_acc[(c, half)][:],
+                    in1=b2_all[:, cols].unsqueeze(1).to_broadcast([P, 2, W2_CHUNK]),
+                    op=ALU.add,
+                )
+            nc.sync.dma_start(out=enc_x_rows[:, :, cols], in_=enc[c][:])
+
+        def turn_pairs(c):
+            cols = slice(c * W2_CHUNK, (c + 1) * W2_CHUNK)
+            pairs = slice(c * CHUNK_PAIRS, (c + 1) * CHUNK_PAIRS)
+            enc_pairs = enc[c][:].rearrange("p b (i e) -> p b i e", e=2)
+            by_cos = product_pool.tile([P, BATCH_TILES, CHUNK_PAIRS, 2], F32, name="by_cos")
+            nc.vector.tensor_tensor(
+                out=by_cos[:],
+                in0=enc_pairs,
+                in1=cos_amp[:, :, pairs].unsqueeze(3).to_broadcast([P, BATCH_TILES, CHUNK_PAIRS, 2]),
+                op=ALU.mult,
+            )
+            by_sin = product_pool.tile([P, 2, BATCH_TILES, CHUNK_PAIRS], F32, name="by_sin")
+            nc.vector.scalar_tensor_tensor(
+                out=by_sin[:, 0, :, :],
+                in0=enc_pairs[:, :, :, 1],
+                scalar=-1.0,
+                in1=sin_amp[:, :, pairs],
+                op0=ALU.mult,
+                op1=ALU.mult,
+            )
+            nc.vector.tensor_tensor(
+                out=by_sin[:, 1, :, :], in0=enc_pairs[:, :, :, 0], in1=sin_amp[:, :, pairs], op=ALU.mult
+            )
+            pred = out_pool.tile([P, BATCH_TILES, CHUNK_PAIRS, 2], F32, name="pred")
+            nc.vector.tensor_tensor(
+                out=pred[:], in0=by_cos[:], in1=by_sin[:].rearrange("p e b i -> p b i e"), op=ALU.add
+            )
+            nc.sync.dma_start(
+                out=enc_pred_rows[:, :, cols], in_=pred[:].rearrange("p b i e -> p b (i e)")
+            )
+
+        def scalar_regroups_ahead(k):
+            if k < n_pieces:
+                scalar_regroups_w1(k)
+            else:
+                scalar_regroups_w2(k - n_pieces)
+
+        for k in range(SCALAR_LEAD):
+            scalar_regroups_ahead(k)
+        vector_regroups_w1(0)
+        for k in range(n_pieces):
+            c, g = divmod(k, PASSES)
+            scalar_regroups_ahead(k + SCALAR_LEAD)
+            if k + 1 < n_pieces:
+                vector_regroups_w1(k + 1)
+            if k + W1_RAW_BUFS < n_pieces:
+                load_w1_piece(k + W1_RAW_BUFS)
+            multiply_w1_piece(k)
+            if g == PASSES - 1:
+                tanh_h(c)
+            if c > 0 and g == PASSES - 2:
+                regroup_h(c - 1)
+            if c > 0 and g == PASSES - 1:
+                quantise_h(c - 1)
+        b2_all = keep.tile([P, LATENT], BF16)
+        nc.sync.dma_start(out=b2_all[:], in_=b_enc2.partition_broadcast(P))
+
+        last = W1_CHUNKS - 1
+        for job in range(SCALAR_LEAD, PASSES):
+            scalar_regroups_w2(job)
+        quantise_w2(0, 0)
+        nc.vector.tensor_tensor(out=sin_amp[:], in0=sin_amp[:], in1=power[:], op=ALU.mult)
+        regroup_h(last)
+        quantise_w2(0, 2)
+        quantise_h(last)
+        multiply_w2_chunk(0)
+        nc.vector.tensor_tensor(out=cos_amp[:], in0=cos_amp[:], in1=power[:], op=ALU.mult)
+
+        for c in range(W2_CHUNKS):
+            if c + 1 < W2_CHUNKS:
+                for g in range(PASSES):
+                    scalar_regroups_w2((c + 1) * PASSES + g)
+                quantise_w2(c + 1, 0)
+                quantise_w2(c + 1, 2)
+            add_b2(c)
+            if c + 1 < W2_CHUNKS:
+                multiply_w2_chunk(c + 1)
+            turn_pairs(c)

@@ -77,6 +77,27 @@ def tile_koopmanae_pa_kernel(
             out=rows[HID_TILES : HID_TILES + BATCH_TILES, :],
             in_=delta_t.rearrange("(b p) -> b p", p=P),
         )
+        FREQ_ROW, AMPL_ROW, B2_ROW = 0, 1, 2
+        vectors = keep.tile([P, PAIRS], BF16)
+        nc.vector.memset(vectors[:], 0.0)
+        nc.sync.dma_start(
+            out=vectors[FREQ_ROW : FREQ_ROW + 1, :], in_=frequencies.rearrange("(r n) -> r n", r=1)
+        )
+        nc.sync.dma_start(
+            out=vectors[AMPL_ROW : AMPL_ROW + 1, :], in_=amplitudes.rearrange("(r n) -> r n", r=1)
+        )
+        nc.sync.dma_start(out=vectors[B2_ROW : B2_ROW + 2, :], in_=b_enc2.rearrange("(r n) -> r n", r=2))
+
+        def spread_row(r):
+            bank = psum_h.tile([P, PAIRS], F32, name="spread", tag="h_acc")
+            nc.tensor.matmul(
+                out=bank[:],
+                lhsT=ident_bf16[:, r : r + 1].to_broadcast([P, P]),
+                rhs=vectors[:],
+                start=True,
+                stop=True,
+            )
+            return bank
 
         w1_rows = W_enc1.rearrange("(g p j) n -> g p j n", p=P, j=PACK)
         w2_rows = W_enc2.rearrange("(g t p) n -> g p t n", t=PACK, p=P)
@@ -90,19 +111,16 @@ def tile_koopmanae_pa_kernel(
             nc.sync.dma_start(
                 out=w1_raw[k][:], in_=w1_rows[g, :, :, c * W1_CHUNK : (c + 1) * W1_CHUNK]
             )
-            if g == PASSES - 1:
-                nc.sync.dma_start(out=w2_raw[:, c, :, :], in_=w2_rows[c])
+            if k == n_pieces - 1:
+                for w2_pass in range(PASSES):
+                    nc.sync.dma_start(out=w2_raw[:, w2_pass, :, :], in_=w2_rows[w2_pass])
 
-        with tc.tile_pool(name="early", bufs=1) as early, tc.tile_pool(name="turns", bufs=2) as turns:
+        with tc.tile_pool(name="early", bufs=1) as early:
             x_sb = early.tile([P, BATCH_TILES, D_IN], BF16)
             for b in range(BATCH_TILES):
                 nc.sync.dma_start(out=x_sb[:, b, :], in_=x[b * P : (b + 1) * P, :])
             for k in range(W1_RAW_BUFS):
                 load_w1_piece(k)
-            freq_all = early.tile([P, PAIRS], BF16)
-            nc.scalar.dma_start(out=freq_all[:], in_=frequencies.partition_broadcast(P))
-            ampl_all = early.tile([P, PAIRS], BF16)
-            nc.scalar.dma_start(out=ampl_all[:], in_=amplitudes.partition_broadcast(P))
 
             columns_ps = psum_small.tile([P, P], BF16, tag="small")
             nc.tensor.transpose(columns_ps[:], rows[:], ident_bf16[:])
@@ -111,8 +129,13 @@ def tile_koopmanae_pa_kernel(
             b1_col = columns[:, 0:HID_TILES]
             dt_col = columns[:, HID_TILES : HID_TILES + BATCH_TILES]
 
+            freq_all = early.tile([P, PAIRS], BF16)
+            nc.vector.tensor_copy(out=freq_all[:], in_=spread_row(FREQ_ROW)[:])
             ln_ampl = early.tile([P, PAIRS], F32)
-            nc.scalar.activation(out=ln_ampl[:], in_=ampl_all[:], func=ACT.Ln)
+            nc.scalar.activation(out=ln_ampl[:], in_=spread_row(AMPL_ROW)[:], func=ACT.Ln)
+            b2_all = keep.tile([P, 2, PAIRS], BF16)
+            for r in range(2):
+                nc.scalar.copy(out=b2_all[:, r, :], in_=spread_row(B2_ROW + r)[:])
             power = keep.tile([P, BATCH_TILES, PAIRS], F32)
             for b in range(BATCH_TILES):
                 nc.scalar.activation(
@@ -123,33 +146,45 @@ def tile_koopmanae_pa_kernel(
             nc.vector.tensor_scalar(
                 out=dt_turns[:], in0=dt_col, scalar1=1.0 / (2.0 * math.pi), scalar2=None, op0=ALU.mult
             )
+            shifted = early.tile([P, BATCH_TILES, PAIRS], F32)
+            whole = early.tile([P, BATCH_TILES, PAIRS], F32)
             part = early.tile([P, BATCH_TILES, PAIRS], F32)
+            minus_abs_part = early.tile([P, BATCH_TILES, PAIRS], F32)
             for b in range(BATCH_TILES):
-                shifted = turns.tile([P, PAIRS], F32)
                 nc.vector.tensor_scalar(
-                    out=shifted[:],
+                    out=shifted[:, b, :],
                     in0=freq_all[:],
                     scalar1=dt_turns[:, b : b + 1],
                     scalar2=ROUND_TO_WHOLE,
                     op0=ALU.mult,
                     op1=ALU.add,
                 )
-                whole = turns.tile([P, PAIRS], F32)
+            for two in (slice(0, 2), slice(2, 4)):
                 nc.vector.tensor_scalar(
-                    out=whole[:], in0=shifted[:], scalar1=ROUND_TO_WHOLE, scalar2=None, op0=ALU.subtract
+                    out=whole[:, two, :],
+                    in0=shifted[:, two, :],
+                    scalar1=ROUND_TO_WHOLE,
+                    scalar2=None,
+                    op0=ALU.subtract,
                 )
+            for b in range(BATCH_TILES):
                 nc.vector.scalar_tensor_tensor(
                     out=part[:, b, :],
                     in0=freq_all[:],
                     scalar=dt_turns[:, b : b + 1],
-                    in1=whole[:],
+                    in1=whole[:, b, :],
                     op0=ALU.mult,
                     op1=ALU.subtract,
                 )
-            minus_abs_part = early.tile([P, BATCH_TILES, PAIRS], F32)
-            nc.vector.scalar_tensor_tensor(
-                out=minus_abs_part[:], in0=part[:], scalar=-1.0, in1=part[:], op0=ALU.mult, op1=ALU.min
-            )
+            for two in (slice(0, 2), slice(2, 4)):
+                nc.vector.scalar_tensor_tensor(
+                    out=minus_abs_part[:, two, :],
+                    in0=part[:, two, :],
+                    scalar=-1.0,
+                    in1=part[:, two, :],
+                    op0=ALU.mult,
+                    op1=ALU.min,
+                )
             sin_amp = keep.tile([P, BATCH_TILES, PAIRS], F32)
             nc.scalar.activation(out=sin_amp[:], in_=part[:], func=ACT.Sin, scale=2.0 * math.pi)
             cos_amp = keep.tile([P, BATCH_TILES, PAIRS], F32)
@@ -181,7 +216,7 @@ def tile_koopmanae_pa_kernel(
                     .rearrange("p (b u) -> p b u", u=2)
                 )
                 for half in range(2):
-                    xt = psum_small.tile([P, 2, 2 * P], F32, tag="small")
+                    xt = psum_h.tile([P, 2, 2 * P], F32, tag="h_acc")
                     for j in range(2):
                         words = (
                             x_sb[:, 2 * half + j, :]
@@ -311,12 +346,13 @@ def tile_koopmanae_pa_kernel(
 
         def add_b2(c):
             cols = slice(c * W2_CHUNK, (c + 1) * W2_CHUNK)
+            b2_row = b2_all[:].rearrange("p r n -> p (r n)")
             enc[c] = out_pool.tile([P, BATCH_TILES, W2_CHUNK], F32, name="enc")
             for half in range(2):
                 nc.vector.tensor_tensor(
                     out=enc[c][:, 2 * half : 2 * half + 2, :],
                     in0=enc_acc[(c, half)][:],
-                    in1=b2_all[:, cols].unsqueeze(1).to_broadcast([P, 2, W2_CHUNK]),
+                    in1=b2_row[:, cols].unsqueeze(1).to_broadcast([P, 2, W2_CHUNK]),
                     op=ALU.add,
                 )
             nc.sync.dma_start(out=enc_x_rows[:, :, cols], in_=enc[c][:])
@@ -375,8 +411,6 @@ def tile_koopmanae_pa_kernel(
                 regroup_h(c - 1)
             if c > 0 and g == PASSES - 1:
                 quantise_h(c - 1)
-        b2_all = keep.tile([P, LATENT], BF16)
-        nc.sync.dma_start(out=b2_all[:], in_=b_enc2.partition_broadcast(P))
 
         last = W1_CHUNKS - 1
         for job in range(SCALAR_LEAD, PASSES):
@@ -390,12 +424,11 @@ def tile_koopmanae_pa_kernel(
         nc.vector.tensor_tensor(out=cos_amp[:], in0=cos_amp[:], in1=power[:], op=ALU.mult)
 
         for c in range(W2_CHUNKS):
+            add_b2(c)
             if c + 1 < W2_CHUNKS:
                 for g in range(PASSES):
                     scalar_regroups_w2((c + 1) * PASSES + g)
                 quantise_w2(c + 1, 0)
                 quantise_w2(c + 1, 2)
-            add_b2(c)
-            if c + 1 < W2_CHUNKS:
                 multiply_w2_chunk(c + 1)
             turn_pairs(c)

@@ -8,6 +8,7 @@ F32 = mybir.dt.float32
 BF16 = mybir.dt.bfloat16
 U32 = mybir.dt.uint32
 U8 = mybir.dt.uint8
+I32 = mybir.dt.int32
 FP8X4 = mybir.dt.float8_e4m3fn_x4
 ALU = mybir.AluOpType
 ACT = mybir.ActivationFunctionType
@@ -28,11 +29,10 @@ W2_CHUNK = 256
 W2_CHUNKS = LATENT // W2_CHUNK
 CHUNK_PAIRS = W2_CHUNK // 2
 
-W1_VECTOR_COLS = 288
+W1_VECTOR_CHUNKS = 1
+W1_VECTOR_COLS = 256
 SCALAR_LEAD = 3
-W1_RAW_BUFS = 6
-
-ROUND_TO_WHOLE = 1.5 * 2.0**23
+W1_RAW_BUFS = 8
 
 FLOPS = 2 * BATCH * D_IN * HID + 2 * BATCH * HID * LATENT
 
@@ -56,7 +56,7 @@ def tile_koopmanae_pa_kernel(
         grouped_pool = ctx.enter_context(tc.tile_pool(name="grouped", bufs=3))
         w1_mx_pool = ctx.enter_context(tc.tile_pool(name="w1_mx", bufs=2))
         psum_h = ctx.enter_context(tc.psum_pool(name="psum_h", bufs=6))
-        psum_small = ctx.enter_context(tc.psum_pool(name="psum_small", bufs=2))
+        psum_stage = ctx.enter_context(tc.psum_pool(name="psum_stage", bufs=2))
 
         x_codes = keep.tile([P, PASSES, BATCH], U32, align_bytes=64)
         x_scales = keep.tile([P, PASSES, BATCH], U8, align_bytes=64)
@@ -115,146 +115,34 @@ def tile_koopmanae_pa_kernel(
                 for w2_pass in range(PASSES):
                     nc.sync.dma_start(out=w2_raw[:, w2_pass, :, :], in_=w2_rows[w2_pass])
 
-        with tc.tile_pool(name="early", bufs=1) as early:
-            x_sb = early.tile([P, BATCH_TILES, D_IN], BF16)
-            for b in range(BATCH_TILES):
-                nc.sync.dma_start(out=x_sb[:, b, :], in_=x[b * P : (b + 1) * P, :])
-            for k in range(W1_RAW_BUFS):
-                load_w1_piece(k)
-
-            columns_ps = psum_small.tile([P, P], BF16, tag="small")
-            nc.tensor.transpose(columns_ps[:], rows[:], ident_bf16[:])
-            columns = keep.tile([P, HID_TILES + BATCH_TILES], F32)
-            nc.vector.tensor_copy(out=columns[:], in_=columns_ps[:, 0 : HID_TILES + BATCH_TILES])
-            b1_col = columns[:, 0:HID_TILES]
-            dt_col = columns[:, HID_TILES : HID_TILES + BATCH_TILES]
-
-            freq_all = early.tile([P, PAIRS], BF16)
-            nc.vector.tensor_copy(out=freq_all[:], in_=spread_row(FREQ_ROW)[:])
-            ln_ampl = early.tile([P, PAIRS], F32)
-            nc.scalar.activation(out=ln_ampl[:], in_=spread_row(AMPL_ROW)[:], func=ACT.Ln)
-            b2_all = keep.tile([P, 2, PAIRS], BF16)
-            for r in range(2):
-                nc.scalar.copy(out=b2_all[:, r, :], in_=spread_row(B2_ROW + r)[:])
-            power = keep.tile([P, BATCH_TILES, PAIRS], F32)
-            for b in range(BATCH_TILES):
-                nc.scalar.activation(
-                    out=power[:, b, :], in_=ln_ampl[:], func=ACT.Exp, scale=dt_col[:, b : b + 1]
-                )
-
-            dt_turns = keep.tile([P, BATCH_TILES], F32)
-            nc.vector.tensor_scalar(
-                out=dt_turns[:], in0=dt_col, scalar1=1.0 / (2.0 * math.pi), scalar2=None, op0=ALU.mult
-            )
-            shifted = early.tile([P, BATCH_TILES, PAIRS], F32)
-            whole = early.tile([P, BATCH_TILES, PAIRS], F32)
-            part = early.tile([P, BATCH_TILES, PAIRS], F32)
-            minus_abs_part = early.tile([P, BATCH_TILES, PAIRS], F32)
-            for b in range(BATCH_TILES):
-                nc.vector.tensor_scalar(
-                    out=shifted[:, b, :],
-                    in0=freq_all[:],
-                    scalar1=dt_turns[:, b : b + 1],
-                    scalar2=ROUND_TO_WHOLE,
-                    op0=ALU.mult,
-                    op1=ALU.add,
-                )
-            for two in (slice(0, 2), slice(2, 4)):
-                nc.vector.tensor_scalar(
-                    out=whole[:, two, :],
-                    in0=shifted[:, two, :],
-                    scalar1=ROUND_TO_WHOLE,
-                    scalar2=None,
-                    op0=ALU.subtract,
-                )
-            for b in range(BATCH_TILES):
-                nc.vector.scalar_tensor_tensor(
-                    out=part[:, b, :],
-                    in0=freq_all[:],
-                    scalar=dt_turns[:, b : b + 1],
-                    in1=whole[:, b, :],
-                    op0=ALU.mult,
-                    op1=ALU.subtract,
-                )
-            for two in (slice(0, 2), slice(2, 4)):
-                nc.vector.scalar_tensor_tensor(
-                    out=minus_abs_part[:, two, :],
-                    in0=part[:, two, :],
-                    scalar=-1.0,
-                    in1=part[:, two, :],
-                    op0=ALU.mult,
-                    op1=ALU.min,
-                )
-            sin_amp = keep.tile([P, BATCH_TILES, PAIRS], F32)
-            nc.scalar.activation(out=sin_amp[:], in_=part[:], func=ACT.Sin, scale=2.0 * math.pi)
-            cos_amp = keep.tile([P, BATCH_TILES, PAIRS], F32)
-            nc.scalar.activation(
-                out=cos_amp[:],
-                in_=minus_abs_part[:],
-                func=ACT.Sin,
-                scale=2.0 * math.pi,
-                bias=math.pi / 2.0,
-            )
-
-            x_grouped = {}
-
-            def quantise_x(g):
-                nc.vector.quantize_mx(
-                    out=x_codes[:, g, :].bitcast(FP8X4),
-                    scales=x_scales[:, g, :],
-                    in_=x_grouped[g][:].rearrange("p b t -> p (b t)"),
-                )
-
-            for g in range(PASSES):
-                x_grouped[g] = grouped_pool.tile(
-                    [P, BATCH, PACK], BF16, align_bytes=64, name="x_grouped", tag="grouped"
-                )
-                x_grouped_words = (
-                    x_grouped[g][:]
-                    .rearrange("p b t -> p (b t)")
-                    .bitcast(F32)
-                    .rearrange("p (b u) -> p b u", u=2)
-                )
-                for half in range(2):
-                    xt = psum_h.tile([P, 2, 2 * P], F32, tag="h_acc")
-                    for j in range(2):
-                        words = (
-                            x_sb[:, 2 * half + j, :]
-                            .bitcast(F32)
-                            .rearrange("p (g q u) -> p g u q", g=PASSES, u=2)
-                        )
-                        for u in range(2):
-                            nc.tensor.transpose(
-                                xt[:, u, j * P : (j + 1) * P], words[:, g, u, :], ident_f32[:]
-                            )
-                    nc.vector.tensor_copy(
-                        out=x_grouped_words[:, half * 2 * P : (half + 1) * 2 * P, :],
-                        in_=xt[:].rearrange("p u b -> p b u"),
-                    )
-                if g > 0:
-                    quantise_x(g - 1)
-            quantise_x(PASSES - 1)
-
-        h_pool = ctx.enter_context(tc.tile_pool(name="h", bufs=2))
-        out_pool = ctx.enter_context(tc.tile_pool(name="out", bufs=2))
-        product_pool = ctx.enter_context(tc.tile_pool(name="product", bufs=1))
-
         w1_grouped = {}
         w1_mx = {}
         h_acc = {}
         h_planes = {}
         h_grouped = {}
-        vector_cols = slice(0, W1_VECTOR_COLS)
-        scalar_cols = slice(W1_VECTOR_COLS, W1_CHUNK)
+        staged_cols = slice(W1_VECTOR_COLS, W1_CHUNK)
 
-        def scalar_regroups_w1(k):
+        def stage_w1(k):
             w1_grouped[k] = w1_grouped_pool.tile(
                 [P, W1_CHUNK, PACK], BF16, align_bytes=64, name="w1_grouped"
             )
-            regroup(nc.scalar.copy, w1_grouped[k][:, scalar_cols, :], w1_raw[k][:, :, scalar_cols])
+            if k // PASSES < W1_VECTOR_CHUNKS:
+                return
+            bank = psum_stage.tile([P, W1_CHUNK - W1_VECTOR_COLS, PACK], BF16, name="bank", tag="stage")
+            for j in range(2):
+                first = W1_VECTOR_COLS + j * P
+                nc.tensor.matmul(
+                    out=bank[:, j * P : (j + 1) * P, :],
+                    lhsT=ident_bf16[:],
+                    rhs=w1_raw[k][:, :, first : first + P].rearrange("p t n -> p n t"),
+                    start=True,
+                    stop=True,
+                )
+            nc.scalar.copy(out=w1_grouped[k][:, staged_cols, :], in_=bank[:])
 
         def vector_regroups_w1(k):
-            regroup(nc.vector.tensor_copy, w1_grouped[k][:, vector_cols, :], w1_raw[k][:, :, vector_cols])
+            cols = slice(0, W1_CHUNK if k // PASSES < W1_VECTOR_CHUNKS else W1_VECTOR_COLS)
+            regroup(nc.vector.tensor_copy, w1_grouped[k][:, cols, :], w1_raw[k][:, :, cols])
 
         def multiply_w1_piece(k):
             c, g = divmod(k, PASSES)
@@ -303,6 +191,116 @@ def tile_koopmanae_pa_kernel(
                 in_=h_grouped[c][:].rearrange("p b t -> p (b t)"),
             )
 
+        with tc.tile_pool(name="early", bufs=1) as early:
+            x_sb = early.tile([P, BATCH_TILES, D_IN], BF16)
+            for b in range(BATCH_TILES):
+                nc.sync.dma_start(out=x_sb[:, b, :], in_=x[b * P : (b + 1) * P, :])
+            for k in range(W1_RAW_BUFS):
+                load_w1_piece(k)
+
+            columns_ps = psum_stage.tile([P, P], BF16, name="columns_ps", tag="stage")
+            nc.tensor.transpose(columns_ps[:], rows[:], ident_bf16[:])
+            columns = keep.tile([P, HID_TILES + BATCH_TILES], F32)
+            nc.vector.tensor_copy(out=columns[:], in_=columns_ps[:, 0 : HID_TILES + BATCH_TILES])
+            b1_col = columns[:, 0:HID_TILES]
+            dt_col = columns[:, HID_TILES : HID_TILES + BATCH_TILES]
+
+            freq_all = early.tile([P, PAIRS], BF16)
+            nc.vector.tensor_copy(out=freq_all[:], in_=spread_row(FREQ_ROW)[:])
+            ln_ampl = early.tile([P, PAIRS], F32)
+            nc.scalar.activation(out=ln_ampl[:], in_=spread_row(AMPL_ROW)[:], func=ACT.Ln)
+            b2_all = keep.tile([P, 2, PAIRS], BF16)
+            for r in range(2):
+                nc.scalar.copy(out=b2_all[:, r, :], in_=spread_row(B2_ROW + r)[:])
+
+            dt_turns = keep.tile([P, BATCH_TILES], F32)
+            nc.vector.tensor_scalar(
+                out=dt_turns[:], in0=dt_col, scalar1=1.0 / (2.0 * math.pi), scalar2=None, op0=ALU.mult
+            )
+            whole = early.tile([P, BATCH_TILES, PAIRS], I32)
+            sin_amp = keep.tile([P, BATCH_TILES, PAIRS], F32)
+            cos_amp = keep.tile([P, BATCH_TILES, PAIRS], F32)
+            power = keep.tile([P, BATCH_TILES, PAIRS], F32)
+            for b in range(BATCH_TILES):
+                nc.vector.tensor_scalar(
+                    out=whole[:, b, :],
+                    in0=freq_all[:],
+                    scalar1=dt_turns[:, b : b + 1],
+                    scalar2=None,
+                    op0=ALU.mult,
+                )
+            for b in range(BATCH_TILES):
+                nc.vector.scalar_tensor_tensor(
+                    out=sin_amp[:, b, :],
+                    in0=freq_all[:],
+                    scalar=dt_turns[:, b : b + 1],
+                    in1=whole[:, b, :],
+                    op0=ALU.mult,
+                    op1=ALU.subtract,
+                )
+
+            x_grouped = early.tile([P, PASSES, BATCH, PACK], BF16, align_bytes=64)
+            x_grouped_words = (
+                x_grouped[:]
+                .rearrange("p g b t -> p (g b t)")
+                .bitcast(F32)
+                .rearrange("p (g b u) -> p g b u", g=PASSES, u=2)
+            )
+            for b in range(BATCH_TILES):
+                words = x_sb[:, b, :].bitcast(F32).rearrange("p (g q u) -> p g u q", g=PASSES, u=2)
+                for half in range(2):
+                    xt = psum_h.tile([P, 2, 2, P], F32, name="xt", tag="h_acc")
+                    for j in range(2):
+                        for u in range(2):
+                            nc.tensor.transpose(
+                                xt[:, j, u, :], words[:, 2 * half + j, u, :], ident_f32[:]
+                            )
+                    nc.scalar.copy(
+                        out=x_grouped_words[:, 2 * half : 2 * half + 2, b * P : (b + 1) * P, :],
+                        in_=xt[:].rearrange("p j u b -> p j b u"),
+                    )
+
+            for b in range(BATCH_TILES):
+                nc.scalar.activation(
+                    out=power[:, b, :], in_=ln_ampl[:], func=ACT.Exp, scale=dt_col[:, b : b + 1]
+                )
+            for k in range(SCALAR_LEAD):
+                stage_w1(k)
+            vector_regroups_w1(0)
+            for g in range(PASSES):
+                nc.vector.quantize_mx(
+                    out=x_codes[:, g, :].bitcast(FP8X4),
+                    scales=x_scales[:, g, :],
+                    in_=x_grouped[:, g, :, :].rearrange("p b t -> p (b t)"),
+                )
+            set_loader = keep.tile([P, 1], F32)
+            nc.scalar.activation(out=set_loader[:], in_=ident_f32[:, 0:1], func=ACT.Silu)
+
+        def take_abs(two):
+            nc.scalar.activation(out=cos_amp[:, two, :], in_=sin_amp[:, two, :], func=ACT.Abs)
+
+        def take_sin(two):
+            nc.scalar.activation(
+                out=sin_amp[:, two, :], in_=sin_amp[:, two, :], func=ACT.Sin, scale=2.0 * math.pi
+            )
+
+        def take_cos(two):
+            nc.scalar.activation(
+                out=cos_amp[:, two, :],
+                in_=cos_amp[:, two, :],
+                func=ACT.Sin,
+                scale=-2.0 * math.pi,
+                bias=math.pi / 2.0,
+            )
+
+        table_steps = [
+            (step, two) for step in (take_abs, take_sin, take_cos) for two in (slice(0, 2), slice(2, 4))
+        ]
+
+        h_pool = ctx.enter_context(tc.tile_pool(name="h", bufs=2))
+        out_pool = ctx.enter_context(tc.tile_pool(name="out", bufs=2))
+        product_pool = ctx.enter_context(tc.tile_pool(name="product", bufs=1))
+
         w2_grouped = {}
         enc_acc = {}
         enc = {}
@@ -330,7 +328,7 @@ def tile_koopmanae_pa_kernel(
 
         def multiply_w2_chunk(c):
             for half in range(2):
-                enc_acc[(c, half)] = psum_small.tile([P, 2, W2_CHUNK], F32, name="enc_acc", tag="small")
+                enc_acc[(c, half)] = psum_h.tile([P, 2, W2_CHUNK], F32, name="enc_acc", tag="h_acc")
                 for j in range(2):
                     batch = slice((2 * half + j) * P, (2 * half + j + 1) * P)
                     for g in range(PASSES):
@@ -388,18 +386,18 @@ def tile_koopmanae_pa_kernel(
                 out=enc_pred_rows[:, :, cols], in_=pred[:].rearrange("p b i e -> p b (i e)")
             )
 
-        def scalar_regroups_ahead(k):
+        def scalar_works_ahead(k):
             if k < n_pieces:
-                scalar_regroups_w1(k)
+                stage_w1(k)
             else:
                 scalar_regroups_w2(k - n_pieces)
 
-        for k in range(SCALAR_LEAD):
-            scalar_regroups_ahead(k)
-        vector_regroups_w1(0)
         for k in range(n_pieces):
             c, g = divmod(k, PASSES)
-            scalar_regroups_ahead(k + SCALAR_LEAD)
+            scalar_works_ahead(k + SCALAR_LEAD)
+            if k < len(table_steps):
+                step, two = table_steps[k]
+                step(two)
             if k + 1 < n_pieces:
                 vector_regroups_w1(k + 1)
             if k + W1_RAW_BUFS < n_pieces:

@@ -31,6 +31,7 @@ CHUNK_PAIRS = W2_CHUNK // 2
 
 W1_VECTOR_CHUNKS = 1
 W1_VECTOR_COLS = 256
+RUN = 8
 SCALAR_LEAD = 3
 W1_RAW_BUFS = 8
 
@@ -132,9 +133,9 @@ def tile_koopmanae_pa_kernel(
             for j in range(2):
                 first = W1_VECTOR_COLS + j * P
                 nc.tensor.matmul(
-                    out=bank[:, j * P : (j + 1) * P, :],
+                    out=bank[:, j * P : (j + 1) * P, :].rearrange("p (c i) t -> p c t i", i=RUN),
                     lhsT=ident_bf16[:],
-                    rhs=w1_raw[k][:, :, first : first + P].rearrange("p t n -> p n t"),
+                    rhs=w1_raw[k][:, :, first : first + P].rearrange("p t (c i) -> p c t i", i=RUN),
                     start=True,
                     stop=True,
                 )

@@ -30,8 +30,7 @@ W2_CHUNKS = LATENT // W2_CHUNK
 CHUNK_PAIRS = W2_CHUNK // 2
 
 W1_VECTOR_CHUNKS = 1
-W1_VECTOR_COLS = 256
-RUN = 8
+W1_VECTOR_COLS = 384
 SCALAR_LEAD = 3
 W1_RAW_BUFS = 8
 
@@ -57,7 +56,7 @@ def tile_koopmanae_pa_kernel(
         grouped_pool = ctx.enter_context(tc.tile_pool(name="grouped", bufs=3))
         w1_mx_pool = ctx.enter_context(tc.tile_pool(name="w1_mx", bufs=2))
         psum_h = ctx.enter_context(tc.psum_pool(name="psum_h", bufs=6))
-        psum_stage = ctx.enter_context(tc.psum_pool(name="psum_stage", bufs=2))
+        psum_stage = ctx.enter_context(tc.psum_pool(name="psum_stage", bufs=1))
 
         x_codes = keep.tile([P, PASSES, BATCH], U32, align_bytes=64)
         x_scales = keep.tile([P, PASSES, BATCH], U8, align_bytes=64)
@@ -127,19 +126,8 @@ def tile_koopmanae_pa_kernel(
             w1_grouped[k] = w1_grouped_pool.tile(
                 [P, W1_CHUNK, PACK], BF16, align_bytes=64, name="w1_grouped"
             )
-            if k // PASSES < W1_VECTOR_CHUNKS:
-                return
-            bank = psum_stage.tile([P, W1_CHUNK - W1_VECTOR_COLS, PACK], BF16, name="bank", tag="stage")
-            for j in range(2):
-                first = W1_VECTOR_COLS + j * P
-                nc.tensor.matmul(
-                    out=bank[:, j * P : (j + 1) * P, :].rearrange("p (c i) t -> p c t i", i=RUN),
-                    lhsT=ident_bf16[:],
-                    rhs=w1_raw[k][:, :, first : first + P].rearrange("p t (c i) -> p c t i", i=RUN),
-                    start=True,
-                    stop=True,
-                )
-            nc.scalar.copy(out=w1_grouped[k][:, staged_cols, :], in_=bank[:])
+            if k // PASSES >= W1_VECTOR_CHUNKS:
+                regroup(nc.scalar.copy, w1_grouped[k][:, staged_cols, :], w1_raw[k][:, :, staged_cols])
 
         def vector_regroups_w1(k):
             cols = slice(0, W1_CHUNK if k // PASSES < W1_VECTOR_CHUNKS else W1_VECTOR_COLS)

@@ -30,9 +30,18 @@ W2_CHUNKS = LATENT // W2_CHUNK
 CHUNK_PAIRS = W2_CHUNK // 2
 
 W1_VECTOR_CHUNKS = 1
-W1_VECTOR_COLS = 384
+RUN = 8
+W1_VECTOR_COLS = 320
+RUN = 8
 SCALAR_LEAD = 3
-W1_RAW_BUFS = 8
+X_SPLIT = 1
+TAIL_FROM = 4
+V_SUMS = 2
+EARLY4 = False
+X_BY_SCALAR = 3
+TABLE_AT = (0, 1, 2, 3, 4, 5, 6, 7, 8)
+TABLE_STEP = 0
+W1_RAW_BUFS = 7
 
 FLOPS = 2 * BATCH * D_IN * HID + 2 * BATCH * HID * LATENT
 
@@ -53,10 +62,10 @@ def tile_koopmanae_pa_kernel(
         keep = ctx.enter_context(tc.tile_pool(name="keep", bufs=1))
         w1_raw_pool = ctx.enter_context(tc.tile_pool(name="w1_raw", bufs=W1_RAW_BUFS))
         w1_grouped_pool = ctx.enter_context(tc.tile_pool(name="w1_grouped", bufs=SCALAR_LEAD + 2))
-        grouped_pool = ctx.enter_context(tc.tile_pool(name="grouped", bufs=3))
+        grouped_pool = ctx.enter_context(tc.tile_pool(name="grouped", bufs=5))
         w1_mx_pool = ctx.enter_context(tc.tile_pool(name="w1_mx", bufs=2))
         psum_h = ctx.enter_context(tc.psum_pool(name="psum_h", bufs=6))
-        psum_stage = ctx.enter_context(tc.psum_pool(name="psum_stage", bufs=1))
+        psum_stage = ctx.enter_context(tc.psum_pool(name="psum_stage", bufs=2))
 
         x_codes = keep.tile([P, PASSES, BATCH], U32, align_bytes=64)
         x_scales = keep.tile([P, PASSES, BATCH], U8, align_bytes=64)
@@ -77,7 +86,7 @@ def tile_koopmanae_pa_kernel(
             out=rows[HID_TILES : HID_TILES + BATCH_TILES, :],
             in_=delta_t.rearrange("(b p) -> b p", p=P),
         )
-        FREQ_ROW, AMPL_ROW, B2_ROW = 0, 1, 2
+        FREQ_ROW, AMPL_ROW = 0, 1
         vectors = keep.tile([P, PAIRS], BF16)
         nc.vector.memset(vectors[:], 0.0)
         nc.sync.dma_start(
@@ -86,7 +95,7 @@ def tile_koopmanae_pa_kernel(
         nc.sync.dma_start(
             out=vectors[AMPL_ROW : AMPL_ROW + 1, :], in_=amplitudes.rearrange("(r n) -> r n", r=1)
         )
-        nc.sync.dma_start(out=vectors[B2_ROW : B2_ROW + 2, :], in_=b_enc2.rearrange("(r n) -> r n", r=2))
+        b2_all = keep.tile([P, LATENT], BF16)
 
         def spread_row(r):
             bank = psum_h.tile([P, PAIRS], F32, name="spread", tag="h_acc")
@@ -114,6 +123,7 @@ def tile_koopmanae_pa_kernel(
             if k == n_pieces - 1:
                 for w2_pass in range(PASSES):
                     nc.sync.dma_start(out=w2_raw[:, w2_pass, :, :], in_=w2_rows[w2_pass])
+                nc.sync.dma_start(out=b2_all[:], in_=b_enc2.partition_broadcast(P))
 
         w1_grouped = {}
         w1_mx = {}
@@ -133,20 +143,32 @@ def tile_koopmanae_pa_kernel(
             cols = slice(0, W1_CHUNK if k // PASSES < W1_VECTOR_CHUNKS else W1_VECTOR_COLS)
             regroup(nc.vector.tensor_copy, w1_grouped[k][:, cols, :], w1_raw[k][:, :, cols])
 
-        def multiply_w1_piece(k):
+        def quantise_x(g):
+            nc.vector.quantize_mx(
+                out=x_codes[:, g, :].bitcast(FP8X4),
+                scales=x_scales[:, g, :],
+                in_=x_grouped[:, g, :, :].rearrange("p b t -> p (b t)"),
+            )
+
+        def quantise_w1(k):
             c, g = divmod(k, PASSES)
             if g == 0:
                 w1_mx[c] = (
                     w1_mx_pool.tile([P, PASSES, W1_CHUNK], U32, align_bytes=64, name="w1_codes"),
                     w1_mx_pool.tile([P, PASSES, W1_CHUNK], U8, align_bytes=64, name="w1_scales"),
                 )
-                h_acc[c] = [psum_h.tile([P, BATCH], F32, name="h_acc") for t in range(PACK)]
             codes, scales = w1_mx[c]
             nc.vector.quantize_mx(
                 out=codes[:, g, :].bitcast(FP8X4),
                 scales=scales[:, g, :],
                 in_=w1_grouped[k][:].rearrange("p n t -> p (n t)"),
             )
+
+        def multiply_w1_piece(k):
+            c, g = divmod(k, PASSES)
+            if g == 0:
+                h_acc[c] = [psum_h.tile([P, BATCH], F32, name="h_acc") for t in range(PACK)]
+            codes, scales = w1_mx[c]
             for t in range(PACK):
                 units = slice(t * P, (t + 1) * P)
                 nc.tensor.matmul_mx(
@@ -182,9 +204,12 @@ def tile_koopmanae_pa_kernel(
 
         with tc.tile_pool(name="early", bufs=1) as early:
             x_sb = early.tile([P, BATCH_TILES, D_IN], BF16)
+            load_w1_piece(0)
             for b in range(BATCH_TILES):
                 nc.sync.dma_start(out=x_sb[:, b, :], in_=x[b * P : (b + 1) * P, :])
-            for k in range(W1_RAW_BUFS):
+                if b == X_SPLIT:
+                    load_w1_piece(1)
+            for k in range(2, W1_RAW_BUFS):
                 load_w1_piece(k)
 
             columns_ps = psum_stage.tile([P, P], BF16, name="columns_ps", tag="stage")
@@ -198,9 +223,6 @@ def tile_koopmanae_pa_kernel(
             nc.vector.tensor_copy(out=freq_all[:], in_=spread_row(FREQ_ROW)[:])
             ln_ampl = early.tile([P, PAIRS], F32)
             nc.scalar.activation(out=ln_ampl[:], in_=spread_row(AMPL_ROW)[:], func=ACT.Ln)
-            b2_all = keep.tile([P, 2, PAIRS], BF16)
-            for r in range(2):
-                nc.scalar.copy(out=b2_all[:, r, :], in_=spread_row(B2_ROW + r)[:])
 
             dt_turns = keep.tile([P, BATCH_TILES], F32)
             nc.vector.tensor_scalar(
@@ -228,13 +250,25 @@ def tile_koopmanae_pa_kernel(
                     op1=ALU.subtract,
                 )
 
-            x_grouped = early.tile([P, PASSES, BATCH, PACK], BF16, align_bytes=64)
+            x_grouped = keep.tile(
+                [P, PASSES, BATCH, PACK], BF16, align_bytes=64, name="x_grouped", tag="x_then_products"
+            )
             x_grouped_words = (
                 x_grouped[:]
                 .rearrange("p g b t -> p (g b t)")
                 .bitcast(F32)
                 .rearrange("p (g b u) -> p g b u", g=PASSES, u=2)
             )
+            def take_power(b):
+                nc.scalar.activation(
+                    out=power[:, b, :], in_=ln_ampl[:], func=ACT.Exp, scale=dt_col[:, b : b + 1]
+                )
+
+            for k in range(SCALAR_LEAD):
+                stage_w1(k)
+            vector_regroups_w1(0)
+            vector_regroups_w1(1)
+            take_power(0)
             for b in range(BATCH_TILES):
                 words = x_sb[:, b, :].bitcast(F32).rearrange("p (g q u) -> p g u q", g=PASSES, u=2)
                 for half in range(2):
@@ -244,51 +278,53 @@ def tile_koopmanae_pa_kernel(
                             nc.tensor.transpose(
                                 xt[:, j, u, :], words[:, 2 * half + j, u, :], ident_f32[:]
                             )
-                    nc.scalar.copy(
+                    copy = nc.scalar.copy if b < X_BY_SCALAR else nc.vector.tensor_copy
+                    copy(
                         out=x_grouped_words[:, 2 * half : 2 * half + 2, b * P : (b + 1) * P, :],
                         in_=xt[:].rearrange("p j u b -> p j b u"),
                     )
+                if b == X_SPLIT:
+                    for other in range(1, BATCH_TILES):
+                        take_power(other)
 
-            for b in range(BATCH_TILES):
-                nc.scalar.activation(
-                    out=power[:, b, :], in_=ln_ampl[:], func=ACT.Exp, scale=dt_col[:, b : b + 1]
-                )
-            for k in range(SCALAR_LEAD):
-                stage_w1(k)
-            vector_regroups_w1(0)
-            for g in range(PASSES):
-                nc.vector.quantize_mx(
-                    out=x_codes[:, g, :].bitcast(FP8X4),
-                    scales=x_scales[:, g, :],
-                    in_=x_grouped[:, g, :, :].rearrange("p b t -> p (b t)"),
-                )
             set_loader = keep.tile([P, 1], F32)
             nc.scalar.activation(out=set_loader[:], in_=ident_f32[:, 0:1], func=ACT.Silu)
 
-        def take_abs(two):
-            nc.scalar.activation(out=cos_amp[:, two, :], in_=sin_amp[:, two, :], func=ACT.Abs)
+        def span(first, last):
+            return slice(first * CHUNK_PAIRS, last * CHUNK_PAIRS)
 
-        def take_sin(two):
+        def take_abs(first, last):
+            s = span(first, last)
+            nc.scalar.activation(out=cos_amp[:, :, s], in_=sin_amp[:, :, s], func=ACT.Abs)
+
+        def take_sin(first, last):
+            s = span(first, last)
             nc.scalar.activation(
-                out=sin_amp[:, two, :], in_=sin_amp[:, two, :], func=ACT.Sin, scale=2.0 * math.pi
+                out=sin_amp[:, :, s], in_=sin_amp[:, :, s], func=ACT.Sin, scale=2.0 * math.pi
             )
 
-        def take_cos(two):
+        def take_cos(first, last):
+            s = span(first, last)
             nc.scalar.activation(
-                out=cos_amp[:, two, :],
-                in_=cos_amp[:, two, :],
+                out=cos_amp[:, :, s],
+                in_=cos_amp[:, :, s],
                 func=ACT.Sin,
                 scale=-2.0 * math.pi,
                 bias=math.pi / 2.0,
             )
 
+        def scale_table(table, first, last):
+            s = span(first, last)
+            nc.vector.tensor_tensor(
+                out=table[:, :, s], in0=table[:, :, s], in1=power[:, :, s], op=ALU.mult
+            )
+
         table_steps = [
-            (step, two) for step in (take_abs, take_sin, take_cos) for two in (slice(0, 2), slice(2, 4))
+            (step, c, min(c + 2, TAIL_FROM)) for c in range(0, TAIL_FROM, 2) for step in (take_abs, take_sin, take_cos)
         ]
 
         h_pool = ctx.enter_context(tc.tile_pool(name="h", bufs=2))
         out_pool = ctx.enter_context(tc.tile_pool(name="out", bufs=2))
-        product_pool = ctx.enter_context(tc.tile_pool(name="product", bufs=1))
 
         w2_grouped = {}
         enc_acc = {}
@@ -333,13 +369,12 @@ def tile_koopmanae_pa_kernel(
 
         def add_b2(c):
             cols = slice(c * W2_CHUNK, (c + 1) * W2_CHUNK)
-            b2_row = b2_all[:].rearrange("p r n -> p (r n)")
             enc[c] = out_pool.tile([P, BATCH_TILES, W2_CHUNK], F32, name="enc")
             for half in range(2):
                 nc.vector.tensor_tensor(
                     out=enc[c][:, 2 * half : 2 * half + 2, :],
                     in0=enc_acc[(c, half)][:],
-                    in1=b2_row[:, cols].unsqueeze(1).to_broadcast([P, 2, W2_CHUNK]),
+                    in1=b2_all[:, cols].unsqueeze(1).to_broadcast([P, 2, W2_CHUNK]),
                     op=ALU.add,
                 )
             nc.sync.dma_start(out=enc_x_rows[:, :, cols], in_=enc[c][:])
@@ -348,14 +383,14 @@ def tile_koopmanae_pa_kernel(
             cols = slice(c * W2_CHUNK, (c + 1) * W2_CHUNK)
             pairs = slice(c * CHUNK_PAIRS, (c + 1) * CHUNK_PAIRS)
             enc_pairs = enc[c][:].rearrange("p b (i e) -> p b i e", e=2)
-            by_cos = product_pool.tile([P, BATCH_TILES, CHUNK_PAIRS, 2], F32, name="by_cos")
+            by_cos = products[:, c % 2, 0, :].rearrange("p (b i e) -> p b i e", b=BATCH_TILES, e=2)
             nc.vector.tensor_tensor(
-                out=by_cos[:],
+                out=by_cos,
                 in0=enc_pairs,
                 in1=cos_amp[:, :, pairs].unsqueeze(3).to_broadcast([P, BATCH_TILES, CHUNK_PAIRS, 2]),
                 op=ALU.mult,
             )
-            by_sin = product_pool.tile([P, 2, BATCH_TILES, CHUNK_PAIRS], F32, name="by_sin")
+            by_sin = products[:, c % 2, 1, :].rearrange("p (e b i) -> p e b i", e=2, b=BATCH_TILES)
             nc.vector.scalar_tensor_tensor(
                 out=by_sin[:, 0, :, :],
                 in0=enc_pairs[:, :, :, 1],
@@ -368,12 +403,27 @@ def tile_koopmanae_pa_kernel(
                 out=by_sin[:, 1, :, :], in0=enc_pairs[:, :, :, 0], in1=sin_amp[:, :, pairs], op=ALU.mult
             )
             pred = out_pool.tile([P, BATCH_TILES, CHUNK_PAIRS, 2], F32, name="pred")
-            nc.vector.tensor_tensor(
-                out=pred[:], in0=by_cos[:], in1=by_sin[:].rearrange("p e b i -> p b i e"), op=ALU.add
-            )
-            nc.sync.dma_start(
-                out=enc_pred_rows[:, :, cols], in_=pred[:].rearrange("p b i e -> p b (i e)")
-            )
+            by_sin_pairs = by_sin.rearrange("p e b i -> p b i e")
+            summed = BATCH_TILES if c == W2_CHUNKS - 1 else V_SUMS
+            if summed < BATCH_TILES:
+                rest = slice(summed, BATCH_TILES)
+                bank = psum_h.tile([P, BATCH_TILES - summed, CHUNK_PAIRS, 2], F32, name="bank", tag="h_acc")
+                nc.tensor.matmul(out=bank[:], lhsT=ident_f32[:], rhs=by_cos[:, rest, :, :], start=True, stop=False)
+                nc.tensor.matmul(out=bank[:], lhsT=ident_f32[:], rhs=by_sin_pairs[:, rest, :, :], start=False, stop=True)
+                nc.scalar.copy(out=pred[:, rest, :, :], in_=bank[:])
+            halves = [slice(0, summed)] if summed < BATCH_TILES else [slice(0, 2), slice(2, 4)]
+            for part in halves:
+                nc.vector.tensor_tensor(
+                    out=pred[:, part, :, :], in0=by_cos[:, part, :, :], in1=by_sin_pairs[:, part, :, :], op=ALU.add
+                )
+                if summed == BATCH_TILES:
+                    nc.sync.dma_start(
+                        out=enc_pred_rows[:, part, cols], in_=pred[:, part, :, :].rearrange("p b i e -> p b (i e)")
+                    )
+            if summed < BATCH_TILES:
+                nc.sync.dma_start(
+                    out=enc_pred_rows[:, :, cols], in_=pred[:].rearrange("p b i e -> p b (i e)")
+                )
 
         def scalar_works_ahead(k):
             if k < n_pieces:
@@ -384,38 +434,64 @@ def tile_koopmanae_pa_kernel(
         for k in range(n_pieces):
             c, g = divmod(k, PASSES)
             scalar_works_ahead(k + SCALAR_LEAD)
-            if k < len(table_steps):
-                step, two = table_steps[k]
-                step(two)
-            if k + 1 < n_pieces:
+            for j in range(len(table_steps)):
+                if TABLE_AT[j] == k:
+                    step, ca, cb = table_steps[j]
+                    step(ca, cb)
+            if 1 <= k < n_pieces - 1:
                 vector_regroups_w1(k + 1)
             if k + W1_RAW_BUFS < n_pieces:
                 load_w1_piece(k + W1_RAW_BUFS)
+            quantise_w1(k)
+            if k < PASSES:
+                quantise_x(k)
             multiply_w1_piece(k)
             if g == PASSES - 1:
                 tanh_h(c)
             if c > 0 and g == PASSES - 2:
+                if c == 2:
+                    scale_table(sin_amp, 0, 2)
+                if c == 3:
+                    scale_table(cos_amp, 0, 2)
                 regroup_h(c - 1)
             if c > 0 and g == PASSES - 1:
                 quantise_h(c - 1)
 
+        def prepare(c):
+            if c >= TAIL_FROM:
+                for step in (take_abs, take_sin, take_cos):
+                    step(c, c + 1)
+            for g in range(PASSES):
+                scalar_regroups_w2(c * PASSES + g)
+
+        products = keep.tile(
+            [P, 2, 2, BATCH_TILES * W2_CHUNK], F32, align_bytes=64, name="products", tag="x_then_products"
+        )
         last = W1_CHUNKS - 1
         for job in range(SCALAR_LEAD, PASSES):
             scalar_regroups_w2(job)
         quantise_w2(0, 0)
-        nc.vector.tensor_tensor(out=sin_amp[:], in0=sin_amp[:], in1=power[:], op=ALU.mult)
+        if TAIL_FROM > 2:
+            scale_table(sin_amp, 2, TAIL_FROM)
+            if EARLY4:
+                scale_table(cos_amp, 2, TAIL_FROM)
         regroup_h(last)
         quantise_w2(0, 2)
         quantise_h(last)
+        prepare(1)
         multiply_w2_chunk(0)
-        nc.vector.tensor_tensor(out=cos_amp[:], in0=cos_amp[:], in1=power[:], op=ALU.mult)
+        if not EARLY4 and TAIL_FROM > 2:
+            scale_table(cos_amp, 2, TAIL_FROM)
 
         for c in range(W2_CHUNKS):
             add_b2(c)
+            if c + 2 < W2_CHUNKS:
+                prepare(c + 2)
             if c + 1 < W2_CHUNKS:
-                for g in range(PASSES):
-                    scalar_regroups_w2((c + 1) * PASSES + g)
                 quantise_w2(c + 1, 0)
                 quantise_w2(c + 1, 2)
                 multiply_w2_chunk(c + 1)
+            if c >= TAIL_FROM:
+                scale_table(sin_amp, c, c + 1)
+                scale_table(cos_amp, c, c + 1)
             turn_pairs(c)

@@ -25,20 +25,24 @@ HID_TILES = HID // P
 
 W1_CHUNK = K_PASS
 W1_CHUNKS = HID // W1_CHUNK
-W2_CHUNK = 256
-W2_CHUNKS = LATENT // W2_CHUNK
-CHUNK_PAIRS = W2_CHUNK // 2
+W2_WIDTHS = (256, 256, 256, 256)
+W2_CHUNKS = len(W2_WIDTHS)
+W2_STARTS = tuple(sum(W2_WIDTHS[:c]) for c in range(W2_CHUNKS + 1))
 
 W1_VECTOR_CHUNKS = 1
 RUN = 8
 W1_VECTOR_COLS = 320
 RUN = 8
 SCALAR_LEAD = 3
-X_SPLIT = 1
+X_FIRST = True
+P_AFTER = (3, 9)
 TAIL_FROM = 4
-V_SUMS = 2
+HALF = 2
+TENSOR_SUMS = (2, 2, 2, 0)
+JOBS = ((0,), (1,), (2,))
 EARLY4 = False
-X_BY_SCALAR = 3
+X_BY_VECTOR = (3,)
+INTER = True
 TABLE_AT = (0, 1, 2, 3, 4, 5, 6, 7, 8)
 TABLE_STEP = 0
 W1_RAW_BUFS = 7
@@ -71,8 +75,8 @@ def tile_koopmanae_pa_kernel(
         x_scales = keep.tile([P, PASSES, BATCH], U8, align_bytes=64)
         h_codes = keep.tile([P, PASSES, BATCH], U32, align_bytes=64)
         h_scales = keep.tile([P, PASSES, BATCH], U8, align_bytes=64)
-        w2_codes = keep.tile([P, W2_CHUNKS, PASSES, W2_CHUNK], U32, align_bytes=64)
-        w2_scales = keep.tile([P, W2_CHUNKS, PASSES, W2_CHUNK], U8, align_bytes=64)
+        w2_codes = keep.tile([P, LATENT * PASSES], U32, align_bytes=64)
+        w2_scales = keep.tile([P, LATENT * PASSES], U8, align_bytes=64)
 
         ident_bf16 = keep.tile([P, P], BF16)
         make_identity(nc, ident_bf16[:])
@@ -204,12 +208,11 @@ def tile_koopmanae_pa_kernel(
 
         with tc.tile_pool(name="early", bufs=1) as early:
             x_sb = early.tile([P, BATCH_TILES, D_IN], BF16)
-            load_w1_piece(0)
             for b in range(BATCH_TILES):
                 nc.sync.dma_start(out=x_sb[:, b, :], in_=x[b * P : (b + 1) * P, :])
-                if b == X_SPLIT:
-                    load_w1_piece(1)
-            for k in range(2, W1_RAW_BUFS):
+                if b in P_AFTER:
+                    load_w1_piece(P_AFTER.index(b))
+            for k in range(sum(1 for b in P_AFTER if b < 4), W1_RAW_BUFS):
                 load_w1_piece(k)
 
             columns_ps = psum_stage.tile([P, P], BF16, name="columns_ps", tag="stage")
@@ -219,15 +222,15 @@ def tile_koopmanae_pa_kernel(
             b1_col = columns[:, 0:HID_TILES]
             dt_col = columns[:, HID_TILES : HID_TILES + BATCH_TILES]
 
+            dt_turns = keep.tile([P, BATCH_TILES], F32)
+            nc.vector.tensor_scalar(
+                out=dt_turns[:], in0=dt_col, scalar1=1.0 / (2.0 * math.pi), scalar2=None, op0=ALU.mult
+            )
             freq_all = early.tile([P, PAIRS], BF16)
             nc.vector.tensor_copy(out=freq_all[:], in_=spread_row(FREQ_ROW)[:])
             ln_ampl = early.tile([P, PAIRS], F32)
             nc.scalar.activation(out=ln_ampl[:], in_=spread_row(AMPL_ROW)[:], func=ACT.Ln)
 
-            dt_turns = keep.tile([P, BATCH_TILES], F32)
-            nc.vector.tensor_scalar(
-                out=dt_turns[:], in0=dt_col, scalar1=1.0 / (2.0 * math.pi), scalar2=None, op0=ALU.mult
-            )
             whole = early.tile([P, BATCH_TILES, PAIRS], I32)
             sin_amp = keep.tile([P, BATCH_TILES, PAIRS], F32)
             cos_amp = keep.tile([P, BATCH_TILES, PAIRS], F32)
@@ -266,8 +269,9 @@ def tile_koopmanae_pa_kernel(
 
             for k in range(SCALAR_LEAD):
                 stage_w1(k)
-            vector_regroups_w1(0)
-            vector_regroups_w1(1)
+            if not X_FIRST:
+                vector_regroups_w1(0)
+                vector_regroups_w1(1)
             take_power(0)
             for b in range(BATCH_TILES):
                 words = x_sb[:, b, :].bitcast(F32).rearrange("p (g q u) -> p g u q", g=PASSES, u=2)
@@ -278,20 +282,19 @@ def tile_koopmanae_pa_kernel(
                             nc.tensor.transpose(
                                 xt[:, j, u, :], words[:, 2 * half + j, u, :], ident_f32[:]
                             )
-                    copy = nc.scalar.copy if b < X_BY_SCALAR else nc.vector.tensor_copy
+                    copy = nc.vector.tensor_copy if b in X_BY_VECTOR else nc.scalar.copy
                     copy(
                         out=x_grouped_words[:, 2 * half : 2 * half + 2, b * P : (b + 1) * P, :],
                         in_=xt[:].rearrange("p j u b -> p j b u"),
                     )
-                if b == X_SPLIT:
-                    for other in range(1, BATCH_TILES):
-                        take_power(other)
+                if b < BATCH_TILES - 1:
+                    take_power(b + 1)
 
             set_loader = keep.tile([P, 1], F32)
             nc.scalar.activation(out=set_loader[:], in_=ident_f32[:, 0:1], func=ACT.Silu)
 
         def span(first, last):
-            return slice(first * CHUNK_PAIRS, last * CHUNK_PAIRS)
+            return slice(W2_STARTS[first] // 2, W2_STARTS[last] // 2)
 
         def take_abs(first, last):
             s = span(first, last)
@@ -320,7 +323,7 @@ def tile_koopmanae_pa_kernel(
             )
 
         table_steps = [
-            (step, c, min(c + 2, TAIL_FROM)) for c in range(0, TAIL_FROM, 2) for step in (take_abs, take_sin, take_cos)
+            (step, ca, cb) for ca, cb in ((0, HALF), (HALF, TAIL_FROM)) for step in (take_abs, take_sin, take_cos)
         ]
 
         h_pool = ctx.enter_context(tc.tile_pool(name="h", bufs=2))
@@ -329,68 +332,91 @@ def tile_koopmanae_pa_kernel(
         w2_grouped = {}
         enc_acc = {}
         enc = {}
+        turned = {}
+        pred = {}
         enc_x_rows = out_1.rearrange("(b p) n -> p b n", p=P)
         enc_pred_rows = out_0.rearrange("(b p) n -> p b n", p=P)
 
+        def per_quantise(c):
+            return 512 // W2_WIDTHS[c]
+
         def scalar_regroups_w2(job):
             c, g = divmod(job, PASSES)
-            if g % 2 == 0:
+            w, q = W2_WIDTHS[c], per_quantise(c)
+            if g % q == 0:
                 w2_grouped[(c, g)] = grouped_pool.tile(
-                    [P, 2, W2_CHUNK, PACK], BF16, align_bytes=64, name="w2_grouped", tag="grouped"
+                    [P, q, w, PACK], BF16, align_bytes=64, name="w2_grouped", tag="grouped"
                 )
             regroup(
                 nc.scalar.copy,
-                w2_grouped[(c, g - g % 2)][:, g % 2, :, :],
-                w2_raw[:, g, :, c * W2_CHUNK : (c + 1) * W2_CHUNK],
+                w2_grouped[(c, g - g % q)][:, g % q, :, :],
+                w2_raw[:, g, :, W2_STARTS[c] : W2_STARTS[c + 1]],
             )
 
-        def quantise_w2(c, first):
-            nc.vector.quantize_mx(
-                out=w2_codes[:, c, first : first + 2, :].rearrange("p g n -> p (g n)").bitcast(FP8X4),
-                scales=w2_scales[:, c, first : first + 2, :].rearrange("p g n -> p (g n)"),
-                in_=w2_grouped[(c, first)][:].rearrange("p g n t -> p (g n t)"),
-            )
+        def quantise_w2(c, firsts=None):
+            q = per_quantise(c)
+            for first in range(0, PASSES, q) if firsts is None else firsts:
+                lo = W2_STARTS[c] * PASSES + first * W2_WIDTHS[c]
+                words = slice(lo, lo + 512)
+                nc.vector.quantize_mx(
+                    out=w2_codes[:, words].bitcast(FP8X4),
+                    scales=w2_scales[:, words],
+                    in_=w2_grouped[(c, first)][:].rearrange("p g n t -> p (g n t)"),
+                )
 
         def multiply_w2_chunk(c):
-            for half in range(2):
-                enc_acc[(c, half)] = psum_h.tile([P, 2, W2_CHUNK], F32, name="enc_acc", tag="h_acc")
-                for j in range(2):
-                    batch = slice((2 * half + j) * P, (2 * half + j + 1) * P)
+            w, q = W2_WIDTHS[c], per_quantise(c)
+            for first in range(0, BATCH_TILES, q):
+                acc = psum_h.tile([P, q, w], F32, name="enc_acc", tag="h_acc")
+                enc_acc[(c, first)] = acc
+                for j in range(q):
+                    batch = slice((first + j) * P, (first + j + 1) * P)
                     for g in range(PASSES):
+                        lo = W2_STARTS[c] * PASSES + g * w
                         nc.tensor.matmul_mx(
-                            out=enc_acc[(c, half)][:, j, :],
+                            out=acc[:, j, :],
                             lhsT=h_codes[:, g, batch].bitcast(FP8X4),
                             lhsT_scale=h_scales[:, g, batch],
-                            rhs=w2_codes[:, c, g, :].bitcast(FP8X4),
-                            rhs_scale=w2_scales[:, c, g, :],
+                            rhs=w2_codes[:, lo : lo + w].bitcast(FP8X4),
+                            rhs_scale=w2_scales[:, lo : lo + w],
                             start=(g == 0),
                             stop=(g == PASSES - 1),
                         )
 
-        def add_b2(c):
-            cols = slice(c * W2_CHUNK, (c + 1) * W2_CHUNK)
-            enc[c] = out_pool.tile([P, BATCH_TILES, W2_CHUNK], F32, name="enc")
-            for half in range(2):
+        def add_b2(c, between):
+            w, q = W2_WIDTHS[c], per_quantise(c)
+            cols = slice(W2_STARTS[c], W2_STARTS[c + 1])
+            enc[c] = out_pool.tile([P, BATCH_TILES, w], F32, name="enc")
+            for first in range(0, BATCH_TILES, q):
+                if first and INTER:
+                    between()
                 nc.vector.tensor_tensor(
-                    out=enc[c][:, 2 * half : 2 * half + 2, :],
-                    in0=enc_acc[(c, half)][:],
-                    in1=b2_all[:, cols].unsqueeze(1).to_broadcast([P, 2, W2_CHUNK]),
+                    out=enc[c][:, first : first + q, :],
+                    in0=enc_acc[(c, first)][:],
+                    in1=b2_all[:, cols].unsqueeze(1).to_broadcast([P, q, w]),
                     op=ALU.add,
                 )
             nc.sync.dma_start(out=enc_x_rows[:, :, cols], in_=enc[c][:])
 
         def turn_pairs(c):
-            cols = slice(c * W2_CHUNK, (c + 1) * W2_CHUNK)
-            pairs = slice(c * CHUNK_PAIRS, (c + 1) * CHUNK_PAIRS)
+            w = W2_WIDTHS[c]
+            cols = slice(W2_STARTS[c], W2_STARTS[c + 1])
+            pairs = span(c, c + 1)
             enc_pairs = enc[c][:].rearrange("p b (i e) -> p b i e", e=2)
-            by_cos = products[:, c % 2, 0, :].rearrange("p (b i e) -> p b i e", b=BATCH_TILES, e=2)
-            nc.vector.tensor_tensor(
-                out=by_cos,
-                in0=enc_pairs,
-                in1=cos_amp[:, :, pairs].unsqueeze(3).to_broadcast([P, BATCH_TILES, CHUNK_PAIRS, 2]),
-                op=ALU.mult,
-            )
-            by_sin = products[:, c % 2, 1, :].rearrange("p (e b i) -> p e b i", e=2, b=BATCH_TILES)
+            size = slice(0, BATCH_TILES * w)
+            by_cos = products[:, c % 2, 0, size].rearrange("p (b i e) -> p b i e", b=BATCH_TILES, e=2)
+            def times_cos(tiles):
+                n = tiles.stop - tiles.start
+                nc.vector.tensor_tensor(
+                    out=by_cos[:, tiles, :, :],
+                    in0=enc_pairs[:, tiles, :, :],
+                    in1=cos_amp[:, tiles, pairs].unsqueeze(3).to_broadcast([P, n, w // 2, 2]),
+                    op=ALU.mult,
+                )
+
+            if c < W2_CHUNKS - 1:
+                times_cos(slice(0, BATCH_TILES))
+            by_sin = products[:, c % 2, 1, size].rearrange("p (e b i) -> p e b i", e=2, b=BATCH_TILES)
             nc.vector.scalar_tensor_tensor(
                 out=by_sin[:, 0, :, :],
                 in0=enc_pairs[:, :, :, 1],
@@ -402,34 +428,54 @@ def tile_koopmanae_pa_kernel(
             nc.vector.tensor_tensor(
                 out=by_sin[:, 1, :, :], in0=enc_pairs[:, :, :, 0], in1=sin_amp[:, :, pairs], op=ALU.mult
             )
-            pred = out_pool.tile([P, BATCH_TILES, CHUNK_PAIRS, 2], F32, name="pred")
-            by_sin_pairs = by_sin.rearrange("p e b i -> p b i e")
-            summed = BATCH_TILES if c == W2_CHUNKS - 1 else V_SUMS
-            if summed < BATCH_TILES:
-                rest = slice(summed, BATCH_TILES)
-                bank = psum_h.tile([P, BATCH_TILES - summed, CHUNK_PAIRS, 2], F32, name="bank", tag="h_acc")
-                nc.tensor.matmul(out=bank[:], lhsT=ident_f32[:], rhs=by_cos[:, rest, :, :], start=True, stop=False)
-                nc.tensor.matmul(out=bank[:], lhsT=ident_f32[:], rhs=by_sin_pairs[:, rest, :, :], start=False, stop=True)
-                nc.scalar.copy(out=pred[:, rest, :, :], in_=bank[:])
-            halves = [slice(0, summed)] if summed < BATCH_TILES else [slice(0, 2), slice(2, 4)]
-            for part in halves:
-                nc.vector.tensor_tensor(
-                    out=pred[:, part, :, :], in0=by_cos[:, part, :, :], in1=by_sin_pairs[:, part, :, :], op=ALU.add
+            if c == W2_CHUNKS - 1:
+                times_cos(slice(0, 2))
+                times_cos(slice(2, 4))
+            turned[c] = (by_cos, by_sin.rearrange("p e b i -> p b i e"))
+
+        def tensor_adds(c):
+            w = W2_WIDTHS[c]
+            by_cos, by_sin_pairs = turned[c]
+            pred[c] = out_pool.tile([P, BATCH_TILES, w // 2, 2], F32, name="pred")
+            tensor_sums = TENSOR_SUMS[c]
+            rest = slice(BATCH_TILES - tensor_sums, BATCH_TILES)
+            if tensor_sums:
+                bank = psum_h.tile([P, tensor_sums, w // 2, 2], F32, name="bank", tag="h_acc")
+                nc.tensor.matmul(
+                    out=bank[:], lhsT=ident_f32[:], rhs=by_cos[:, rest, :, :], start=True, stop=False
                 )
-                if summed == BATCH_TILES:
+                nc.tensor.matmul(
+                    out=bank[:], lhsT=ident_f32[:], rhs=by_sin_pairs[:, rest, :, :], start=False, stop=True
+                )
+                nc.scalar.copy(out=pred[c][:, rest, :, :], in_=bank[:])
+
+        def vector_adds(c):
+            by_cos, by_sin_pairs = turned[c]
+            cols = slice(W2_STARTS[c], W2_STARTS[c + 1])
+            last_chunk = c == W2_CHUNKS - 1
+            for part in (slice(0, 2), slice(2, 4)) if last_chunk else (slice(0, BATCH_TILES - TENSOR_SUMS[c]),):
+                nc.vector.tensor_tensor(
+                    out=pred[c][:, part, :, :],
+                    in0=by_cos[:, part, :, :],
+                    in1=by_sin_pairs[:, part, :, :],
+                    op=ALU.add,
+                )
+                if last_chunk:
                     nc.sync.dma_start(
-                        out=enc_pred_rows[:, part, cols], in_=pred[:, part, :, :].rearrange("p b i e -> p b (i e)")
+                        out=enc_pred_rows[:, part, cols],
+                        in_=pred[c][:, part, :, :].rearrange("p b i e -> p b (i e)"),
                     )
-            if summed < BATCH_TILES:
+            if not last_chunk:
                 nc.sync.dma_start(
-                    out=enc_pred_rows[:, :, cols], in_=pred[:].rearrange("p b i e -> p b (i e)")
+                    out=enc_pred_rows[:, :, cols], in_=pred[c][:].rearrange("p b i e -> p b (i e)")
                 )
 
         def scalar_works_ahead(k):
             if k < n_pieces:
                 stage_w1(k)
             else:
-                scalar_regroups_w2(k - n_pieces)
+                for job in JOBS[k - n_pieces]:
+                    scalar_regroups_w2(job)
 
         for k in range(n_pieces):
             c, g = divmod(k, PASSES)
@@ -438,21 +484,27 @@ def tile_koopmanae_pa_kernel(
                 if TABLE_AT[j] == k:
                     step, ca, cb = table_steps[j]
                     step(ca, cb)
-            if 1 <= k < n_pieces - 1:
+            if X_FIRST:
+                if k < 4:
+                    vector_regroups_w1(k)
+                    quantise_x(k)
+                if 3 <= k < n_pieces - 1:
+                    vector_regroups_w1(k + 1)
+            elif 1 <= k < n_pieces - 1:
                 vector_regroups_w1(k + 1)
             if k + W1_RAW_BUFS < n_pieces:
                 load_w1_piece(k + W1_RAW_BUFS)
             quantise_w1(k)
-            if k < PASSES:
+            if k < PASSES and not X_FIRST:
                 quantise_x(k)
             multiply_w1_piece(k)
             if g == PASSES - 1:
                 tanh_h(c)
             if c > 0 and g == PASSES - 2:
                 if c == 2:
-                    scale_table(sin_amp, 0, 2)
+                    scale_table(sin_amp, 0, HALF)
                 if c == 3:
-                    scale_table(cos_amp, 0, 2)
+                    scale_table(cos_amp, 0, HALF)
                 regroup_h(c - 1)
             if c > 0 and g == PASSES - 1:
                 quantise_h(c - 1)
@@ -464,34 +516,38 @@ def tile_koopmanae_pa_kernel(
             for g in range(PASSES):
                 scalar_regroups_w2(c * PASSES + g)
 
-        products = keep.tile(
-            [P, 2, 2, BATCH_TILES * W2_CHUNK], F32, align_bytes=64, name="products", tag="x_then_products"
-        )
+        products = keep.tile([P, 2, 2, BATCH_TILES * 256], F32, align_bytes=64, name="products", tag="x_then_products")
         last = W1_CHUNKS - 1
-        for job in range(SCALAR_LEAD, PASSES):
+        for job in range(sum(len(j) for j in JOBS), PASSES):
             scalar_regroups_w2(job)
-        quantise_w2(0, 0)
-        if TAIL_FROM > 2:
-            scale_table(sin_amp, 2, TAIL_FROM)
-            if EARLY4:
-                scale_table(cos_amp, 2, TAIL_FROM)
+        quantise_w2(0, (0,))
+        scale_table(sin_amp, HALF, TAIL_FROM)
+        if EARLY4:
+            scale_table(cos_amp, HALF, TAIL_FROM)
         regroup_h(last)
-        quantise_w2(0, 2)
+        quantise_w2(0, (2,))
         quantise_h(last)
         prepare(1)
         multiply_w2_chunk(0)
-        if not EARLY4 and TAIL_FROM > 2:
-            scale_table(cos_amp, 2, TAIL_FROM)
+        if not EARLY4:
+            scale_table(cos_amp, HALF, TAIL_FROM)
 
         for c in range(W2_CHUNKS):
-            add_b2(c)
+            def between():
+                if c + 1 < W2_CHUNKS:
+                    quantise_w2(c + 1, (0,))
+
+            add_b2(c, between)
+            if c > 0:
+                vector_adds(c - 1)
             if c + 2 < W2_CHUNKS:
                 prepare(c + 2)
             if c + 1 < W2_CHUNKS:
-                quantise_w2(c + 1, 0)
-                quantise_w2(c + 1, 2)
+                quantise_w2(c + 1, (2,) if INTER else None)
                 multiply_w2_chunk(c + 1)
             if c >= TAIL_FROM:
                 scale_table(sin_amp, c, c + 1)
                 scale_table(cos_amp, c, c + 1)
             turn_pairs(c)
+            tensor_adds(c)
+        vector_adds(W2_CHUNKS - 1)

@@ -43,6 +43,8 @@ JOBS = ((0,), (1,), (2,))
 EARLY4 = False
 X_BY_VECTOR = (3,)
 INTER = True
+JOB3_V = True
+H_SPLIT = 512
 TABLE_AT = (0, 1, 2, 3, 4, 5, 6, 7, 8)
 TABLE_STEP = 0
 W1_RAW_BUFS = 7
@@ -193,11 +195,15 @@ def tile_koopmanae_pa_kernel(
                     out=h_planes[c][:, t, :], in_=h_acc[c][t][:], func=ACT.Tanh, bias=b1_col[:, m : m + 1]
                 )
 
-        def regroup_h(c):
+        def regroup_h(c, by_vector=BATCH):
             h_grouped[c] = grouped_pool.tile(
                 [P, BATCH, PACK], BF16, align_bytes=64, name="h_grouped", tag="grouped"
             )
-            regroup(nc.vector.tensor_copy, h_grouped[c][:], h_planes[c][:])
+            if by_vector < BATCH:
+                rows_s = slice(by_vector, BATCH)
+                regroup(nc.scalar.copy, h_grouped[c][:, rows_s, :], h_planes[c][:, :, rows_s])
+            rows_v = slice(0, by_vector)
+            regroup(nc.vector.tensor_copy, h_grouped[c][:, rows_v, :], h_planes[c][:, :, rows_v])
 
         def quantise_h(c):
             nc.vector.quantize_mx(
@@ -340,7 +346,7 @@ def tile_koopmanae_pa_kernel(
         def per_quantise(c):
             return 512 // W2_WIDTHS[c]
 
-        def scalar_regroups_w2(job):
+        def regroup_w2(job, copy):
             c, g = divmod(job, PASSES)
             w, q = W2_WIDTHS[c], per_quantise(c)
             if g % q == 0:
@@ -348,7 +354,7 @@ def tile_koopmanae_pa_kernel(
                     [P, q, w, PACK], BF16, align_bytes=64, name="w2_grouped", tag="grouped"
                 )
             regroup(
-                nc.scalar.copy,
+                copy,
                 w2_grouped[(c, g - g % q)][:, g % q, :, :],
                 w2_raw[:, g, :, W2_STARTS[c] : W2_STARTS[c + 1]],
             )
@@ -438,9 +444,9 @@ def tile_koopmanae_pa_kernel(
             by_cos, by_sin_pairs = turned[c]
             pred[c] = out_pool.tile([P, BATCH_TILES, w // 2, 2], F32, name="pred")
             tensor_sums = TENSOR_SUMS[c]
-            rest = slice(BATCH_TILES - tensor_sums, BATCH_TILES)
-            if tensor_sums:
-                bank = psum_h.tile([P, tensor_sums, w // 2, 2], F32, name="bank", tag="h_acc")
+            for lo in range(BATCH_TILES - tensor_sums, BATCH_TILES, 2):
+                rest = slice(lo, min(lo + 2, BATCH_TILES))
+                bank = psum_h.tile([P, rest.stop - lo, w // 2, 2], F32, name="bank", tag="h_acc")
                 nc.tensor.matmul(
                     out=bank[:], lhsT=ident_f32[:], rhs=by_cos[:, rest, :, :], start=True, stop=False
                 )
@@ -453,8 +459,8 @@ def tile_koopmanae_pa_kernel(
             by_cos, by_sin_pairs = turned[c]
             cols = slice(W2_STARTS[c], W2_STARTS[c + 1])
             last_chunk = c == W2_CHUNKS - 1
-            for part in (slice(0, 2), slice(2, 4)) if last_chunk else (slice(0, BATCH_TILES - TENSOR_SUMS[c]),):
-                nc.vector.tensor_tensor(
+            for part in (slice(0, 2), slice(2, 4 - TENSOR_SUMS[c])) if last_chunk else (slice(0, BATCH_TILES - TENSOR_SUMS[c]),):
+                if part.stop > part.start: nc.vector.tensor_tensor(
                     out=pred[c][:, part, :, :],
                     in0=by_cos[:, part, :, :],
                     in1=by_sin_pairs[:, part, :, :],
@@ -475,7 +481,7 @@ def tile_koopmanae_pa_kernel(
                 stage_w1(k)
             else:
                 for job in JOBS[k - n_pieces]:
-                    scalar_regroups_w2(job)
+                    regroup_w2(job, nc.scalar.copy)
 
         for k in range(n_pieces):
             c, g = divmod(k, PASSES)
@@ -514,17 +520,21 @@ def tile_koopmanae_pa_kernel(
                 for step in (take_abs, take_sin, take_cos):
                     step(c, c + 1)
             for g in range(PASSES):
-                scalar_regroups_w2(c * PASSES + g)
+                regroup_w2(c * PASSES + g, nc.scalar.copy)
 
         products = keep.tile([P, 2, 2, BATCH_TILES * 256], F32, align_bytes=64, name="products", tag="x_then_products")
         last = W1_CHUNKS - 1
-        for job in range(sum(len(j) for j in JOBS), PASSES):
-            scalar_regroups_w2(job)
+        if not JOB3_V:
+            for job in range(sum(len(j) for j in JOBS), PASSES):
+                regroup_w2(job, nc.scalar.copy)
         quantise_w2(0, (0,))
         scale_table(sin_amp, HALF, TAIL_FROM)
         if EARLY4:
             scale_table(cos_amp, HALF, TAIL_FROM)
-        regroup_h(last)
+        if JOB3_V:
+            for job in range(sum(len(j) for j in JOBS), PASSES):
+                regroup_w2(job, nc.vector.tensor_copy)
+        regroup_h(last, H_SPLIT)
         quantise_w2(0, (2,))
         quantise_h(last)
         prepare(1)

@@ -31,7 +31,7 @@ W2_STARTS = tuple(sum(W2_WIDTHS[:c]) for c in range(W2_CHUNKS + 1))
 
 W1_VECTOR_CHUNKS = 1
 RUN = 8
-W1_VECTOR_COLS = 320
+W1_VECTOR_COLS = 288
 RUN = 8
 SCALAR_LEAD = 3
 X_FIRST = True

@@ -7,8 +7,8 @@ from concourse.masks import make_identity
 F32 = mybir.dt.float32
 BF16 = mybir.dt.bfloat16
 U32 = mybir.dt.uint32
-U8 = mybir.dt.uint8
 I32 = mybir.dt.int32
+U8 = mybir.dt.uint8
 FP8X4 = mybir.dt.float8_e4m3fn_x4
 ALU = mybir.AluOpType
 ACT = mybir.ActivationFunctionType
@@ -25,37 +25,28 @@ HID_TILES = HID // P
 
 W1_CHUNK = K_PASS
 W1_CHUNKS = HID // W1_CHUNK
-W2_WIDTHS = (256, 256, 256, 256)
-W2_CHUNKS = len(W2_WIDTHS)
-W2_STARTS = tuple(sum(W2_WIDTHS[:c]) for c in range(W2_CHUNKS + 1))
+W1_PIECES = W1_CHUNKS * PASSES
+W2_CHUNK = 256
+W2_CHUNKS = LATENT // W2_CHUNK
+CHUNK_PAIRS = W2_CHUNK // 2
+TILES_PER_BANK = 2
+QUANT_PASSES = 2
 
-W1_VECTOR_CHUNKS = 1
-RUN = 8
 W1_VECTOR_COLS = 288
-RUN = 8
 SCALAR_LEAD = 3
-X_FIRST = True
-P_AFTER = (3, 9)
-TAIL_FROM = 4
-HALF = 2
-TENSOR_SUMS = (2, 2, 2, 0)
-JOBS = ((0,), (1,), (2,))
-EARLY4 = False
-X_BY_VECTOR = (3,)
-INTER = True
-JOB3_V = True
-H_SPLIT = 512
-TABLE_AT = (0, 1, 2, 3, 4, 5, 6, 7, 8)
-TABLE_STEP = 0
 W1_RAW_BUFS = 7
+X_TILES_BY_SCALAR = BATCH_TILES - 1
+SUM_TILES_BY_VECTOR = 2
+RUN = 8
+HALF_PAIRS = (slice(0, PAIRS // 2), slice(PAIRS // 2, PAIRS))
 
 FLOPS = 2 * BATCH * D_IN * HID + 2 * BATCH * HID * LATENT
 
 
 def regroup(copy, grouped, planes):
     copy(
-        out=grouped.rearrange("p (c i) t -> p c t i", i=4),
-        in_=planes.rearrange("p t (c i) -> p c t i", i=4),
+        out=grouped.rearrange("p (c i) t -> p c t i", i=RUN),
+        in_=planes.rearrange("p t (c i) -> p c t i", i=RUN),
     )
 
 
@@ -71,7 +62,7 @@ def tile_koopmanae_pa_kernel(
         grouped_pool = ctx.enter_context(tc.tile_pool(name="grouped", bufs=5))
         w1_mx_pool = ctx.enter_context(tc.tile_pool(name="w1_mx", bufs=2))
         psum_h = ctx.enter_context(tc.psum_pool(name="psum_h", bufs=6))
-        psum_stage = ctx.enter_context(tc.psum_pool(name="psum_stage", bufs=2))
+        psum_stage = ctx.enter_context(tc.psum_pool(name="psum_stage", bufs=1))
 
         x_codes = keep.tile([P, PASSES, BATCH], U32, align_bytes=64)
         x_scales = keep.tile([P, PASSES, BATCH], U8, align_bytes=64)
@@ -117,7 +108,6 @@ def tile_koopmanae_pa_kernel(
         w1_rows = W_enc1.rearrange("(g p j) n -> g p j n", p=P, j=PACK)
         w2_rows = W_enc2.rearrange("(g t p) n -> g p t n", t=PACK, p=P)
         w2_raw = keep.tile([P, PASSES, PACK, LATENT], BF16)
-        n_pieces = W1_CHUNKS * PASSES
         w1_raw = {}
 
         def load_w1_piece(k):
@@ -126,7 +116,7 @@ def tile_koopmanae_pa_kernel(
             nc.sync.dma_start(
                 out=w1_raw[k][:], in_=w1_rows[g, :, :, c * W1_CHUNK : (c + 1) * W1_CHUNK]
             )
-            if k == n_pieces - 1:
+            if k == W1_PIECES - 1:
                 for w2_pass in range(PASSES):
                     nc.sync.dma_start(out=w2_raw[:, w2_pass, :, :], in_=w2_rows[w2_pass])
                 nc.sync.dma_start(out=b2_all[:], in_=b_enc2.partition_broadcast(P))
@@ -136,17 +126,20 @@ def tile_koopmanae_pa_kernel(
         h_acc = {}
         h_planes = {}
         h_grouped = {}
-        staged_cols = slice(W1_VECTOR_COLS, W1_CHUNK)
 
-        def stage_w1(k):
+        def vector_cols(k):
+            return W1_CHUNK if k < PASSES else W1_VECTOR_COLS
+
+        def scalar_regroups_w1(k):
             w1_grouped[k] = w1_grouped_pool.tile(
                 [P, W1_CHUNK, PACK], BF16, align_bytes=64, name="w1_grouped"
             )
-            if k // PASSES >= W1_VECTOR_CHUNKS:
-                regroup(nc.scalar.copy, w1_grouped[k][:, staged_cols, :], w1_raw[k][:, :, staged_cols])
+            if vector_cols(k) < W1_CHUNK:
+                cols = slice(vector_cols(k), W1_CHUNK)
+                regroup(nc.scalar.copy, w1_grouped[k][:, cols, :], w1_raw[k][:, :, cols])
 
         def vector_regroups_w1(k):
-            cols = slice(0, W1_CHUNK if k // PASSES < W1_VECTOR_CHUNKS else W1_VECTOR_COLS)
+            cols = slice(0, vector_cols(k))
             regroup(nc.vector.tensor_copy, w1_grouped[k][:, cols, :], w1_raw[k][:, :, cols])
 
         def quantise_x(g):
@@ -195,15 +188,11 @@ def tile_koopmanae_pa_kernel(
                     out=h_planes[c][:, t, :], in_=h_acc[c][t][:], func=ACT.Tanh, bias=b1_col[:, m : m + 1]
                 )
 
-        def regroup_h(c, by_vector=BATCH):
+        def regroup_h(c):
             h_grouped[c] = grouped_pool.tile(
                 [P, BATCH, PACK], BF16, align_bytes=64, name="h_grouped", tag="grouped"
             )
-            if by_vector < BATCH:
-                rows_s = slice(by_vector, BATCH)
-                regroup(nc.scalar.copy, h_grouped[c][:, rows_s, :], h_planes[c][:, :, rows_s])
-            rows_v = slice(0, by_vector)
-            regroup(nc.vector.tensor_copy, h_grouped[c][:, rows_v, :], h_planes[c][:, :, rows_v])
+            regroup(nc.vector.tensor_copy, h_grouped[c][:], h_planes[c][:])
 
         def quantise_h(c):
             nc.vector.quantize_mx(
@@ -216,9 +205,7 @@ def tile_koopmanae_pa_kernel(
             x_sb = early.tile([P, BATCH_TILES, D_IN], BF16)
             for b in range(BATCH_TILES):
                 nc.sync.dma_start(out=x_sb[:, b, :], in_=x[b * P : (b + 1) * P, :])
-                if b in P_AFTER:
-                    load_w1_piece(P_AFTER.index(b))
-            for k in range(sum(1 for b in P_AFTER if b < 4), W1_RAW_BUFS):
+            for k in range(W1_RAW_BUFS):
                 load_w1_piece(k)
 
             columns_ps = psum_stage.tile([P, P], BF16, name="columns_ps", tag="stage")
@@ -259,6 +246,11 @@ def tile_koopmanae_pa_kernel(
                     op1=ALU.subtract,
                 )
 
+            def take_power(b):
+                nc.scalar.activation(
+                    out=power[:, b, :], in_=ln_ampl[:], func=ACT.Exp, scale=dt_col[:, b : b + 1]
+                )
+
             x_grouped = keep.tile(
                 [P, PASSES, BATCH, PACK], BF16, align_bytes=64, name="x_grouped", tag="x_then_products"
             )
@@ -268,16 +260,8 @@ def tile_koopmanae_pa_kernel(
                 .bitcast(F32)
                 .rearrange("p (g b u) -> p g b u", g=PASSES, u=2)
             )
-            def take_power(b):
-                nc.scalar.activation(
-                    out=power[:, b, :], in_=ln_ampl[:], func=ACT.Exp, scale=dt_col[:, b : b + 1]
-                )
-
             for k in range(SCALAR_LEAD):
-                stage_w1(k)
-            if not X_FIRST:
-                vector_regroups_w1(0)
-                vector_regroups_w1(1)
+                scalar_regroups_w1(k)
             take_power(0)
             for b in range(BATCH_TILES):
                 words = x_sb[:, b, :].bitcast(F32).rearrange("p (g q u) -> p g u q", g=PASSES, u=2)
@@ -288,7 +272,7 @@ def tile_koopmanae_pa_kernel(
                             nc.tensor.transpose(
                                 xt[:, j, u, :], words[:, 2 * half + j, u, :], ident_f32[:]
                             )
-                    copy = nc.vector.tensor_copy if b in X_BY_VECTOR else nc.scalar.copy
+                    copy = nc.scalar.copy if b < X_TILES_BY_SCALAR else nc.vector.tensor_copy
                     copy(
                         out=x_grouped_words[:, 2 * half : 2 * half + 2, b * P : (b + 1) * P, :],
                         in_=xt[:].rearrange("p j u b -> p j b u"),
@@ -299,38 +283,29 @@ def tile_koopmanae_pa_kernel(
             set_loader = keep.tile([P, 1], F32)
             nc.scalar.activation(out=set_loader[:], in_=ident_f32[:, 0:1], func=ACT.Silu)
 
-        def span(first, last):
-            return slice(W2_STARTS[first] // 2, W2_STARTS[last] // 2)
+        def take_abs(half):
+            nc.scalar.activation(out=cos_amp[:, :, half], in_=sin_amp[:, :, half], func=ACT.Abs)
 
-        def take_abs(first, last):
-            s = span(first, last)
-            nc.scalar.activation(out=cos_amp[:, :, s], in_=sin_amp[:, :, s], func=ACT.Abs)
-
-        def take_sin(first, last):
-            s = span(first, last)
+        def take_sin(half):
             nc.scalar.activation(
-                out=sin_amp[:, :, s], in_=sin_amp[:, :, s], func=ACT.Sin, scale=2.0 * math.pi
+                out=sin_amp[:, :, half], in_=sin_amp[:, :, half], func=ACT.Sin, scale=2.0 * math.pi
             )
 
-        def take_cos(first, last):
-            s = span(first, last)
+        def take_cos(half):
             nc.scalar.activation(
-                out=cos_amp[:, :, s],
-                in_=cos_amp[:, :, s],
+                out=cos_amp[:, :, half],
+                in_=cos_amp[:, :, half],
                 func=ACT.Sin,
                 scale=-2.0 * math.pi,
                 bias=math.pi / 2.0,
             )
 
-        def scale_table(table, first, last):
-            s = span(first, last)
+        def scale_table(table, half):
             nc.vector.tensor_tensor(
-                out=table[:, :, s], in0=table[:, :, s], in1=power[:, :, s], op=ALU.mult
+                out=table[:, :, half], in0=table[:, :, half], in1=power[:, :, half], op=ALU.mult
             )
 
-        table_steps = [
-            (step, ca, cb) for ca, cb in ((0, HALF), (HALF, TAIL_FROM)) for step in (take_abs, take_sin, take_cos)
-        ]
+        table_steps = [(step, half) for half in HALF_PAIRS for step in (take_abs, take_sin, take_cos)]
 
         h_pool = ctx.enter_context(tc.tile_pool(name="h", bufs=2))
         out_pool = ctx.enter_context(tc.tile_pool(name="out", bufs=2))
@@ -338,93 +313,82 @@ def tile_koopmanae_pa_kernel(
         w2_grouped = {}
         enc_acc = {}
         enc = {}
-        turned = {}
+        by_cos = {}
+        by_sin = {}
         pred = {}
         enc_x_rows = out_1.rearrange("(b p) n -> p b n", p=P)
         enc_pred_rows = out_0.rearrange("(b p) n -> p b n", p=P)
 
-        def per_quantise(c):
-            return 512 // W2_WIDTHS[c]
+        def chunk_cols(c):
+            return slice(c * W2_CHUNK, (c + 1) * W2_CHUNK)
 
-        def regroup_w2(job, copy):
-            c, g = divmod(job, PASSES)
-            w, q = W2_WIDTHS[c], per_quantise(c)
-            if g % q == 0:
-                w2_grouped[(c, g)] = grouped_pool.tile(
-                    [P, q, w, PACK], BF16, align_bytes=64, name="w2_grouped", tag="grouped"
+        def regroup_w2(c, g, copy):
+            first = g - g % QUANT_PASSES
+            if g == first:
+                w2_grouped[(c, first)] = grouped_pool.tile(
+                    [P, QUANT_PASSES, W2_CHUNK, PACK], BF16, align_bytes=64, name="w2_grouped", tag="grouped"
                 )
-            regroup(
-                copy,
-                w2_grouped[(c, g - g % q)][:, g % q, :, :],
-                w2_raw[:, g, :, W2_STARTS[c] : W2_STARTS[c + 1]],
+            regroup(copy, w2_grouped[(c, first)][:, g - first, :, :], w2_raw[:, g, :, chunk_cols(c)])
+
+        def scalar_regroups_w2_chunk(c):
+            for g in range(PASSES):
+                regroup_w2(c, g, nc.scalar.copy)
+
+        def quantise_w2(c, first):
+            start = (c * PASSES + first) * W2_CHUNK
+            words = slice(start, start + QUANT_PASSES * W2_CHUNK)
+            nc.vector.quantize_mx(
+                out=w2_codes[:, words].bitcast(FP8X4),
+                scales=w2_scales[:, words],
+                in_=w2_grouped[(c, first)][:].rearrange("p g n t -> p (g n t)"),
             )
 
-        def quantise_w2(c, firsts=None):
-            q = per_quantise(c)
-            for first in range(0, PASSES, q) if firsts is None else firsts:
-                lo = W2_STARTS[c] * PASSES + first * W2_WIDTHS[c]
-                words = slice(lo, lo + 512)
-                nc.vector.quantize_mx(
-                    out=w2_codes[:, words].bitcast(FP8X4),
-                    scales=w2_scales[:, words],
-                    in_=w2_grouped[(c, first)][:].rearrange("p g n t -> p (g n t)"),
-                )
-
         def multiply_w2_chunk(c):
-            w, q = W2_WIDTHS[c], per_quantise(c)
-            for first in range(0, BATCH_TILES, q):
-                acc = psum_h.tile([P, q, w], F32, name="enc_acc", tag="h_acc")
+            for first in range(0, BATCH_TILES, TILES_PER_BANK):
+                acc = psum_h.tile([P, TILES_PER_BANK, W2_CHUNK], F32, name="enc_acc", tag="h_acc")
                 enc_acc[(c, first)] = acc
-                for j in range(q):
+                for j in range(TILES_PER_BANK):
                     batch = slice((first + j) * P, (first + j + 1) * P)
                     for g in range(PASSES):
-                        lo = W2_STARTS[c] * PASSES + g * w
+                        start = (c * PASSES + g) * W2_CHUNK
+                        words = slice(start, start + W2_CHUNK)
                         nc.tensor.matmul_mx(
                             out=acc[:, j, :],
                             lhsT=h_codes[:, g, batch].bitcast(FP8X4),
                             lhsT_scale=h_scales[:, g, batch],
-                            rhs=w2_codes[:, lo : lo + w].bitcast(FP8X4),
-                            rhs_scale=w2_scales[:, lo : lo + w],
+                            rhs=w2_codes[:, words].bitcast(FP8X4),
+                            rhs_scale=w2_scales[:, words],
                             start=(g == 0),
                             stop=(g == PASSES - 1),
                         )
 
-        def add_b2(c, between):
-            w, q = W2_WIDTHS[c], per_quantise(c)
-            cols = slice(W2_STARTS[c], W2_STARTS[c + 1])
-            enc[c] = out_pool.tile([P, BATCH_TILES, w], F32, name="enc")
-            for first in range(0, BATCH_TILES, q):
-                if first and INTER:
-                    between()
-                nc.vector.tensor_tensor(
-                    out=enc[c][:, first : first + q, :],
-                    in0=enc_acc[(c, first)][:],
-                    in1=b2_all[:, cols].unsqueeze(1).to_broadcast([P, q, w]),
-                    op=ALU.add,
-                )
-            nc.sync.dma_start(out=enc_x_rows[:, :, cols], in_=enc[c][:])
+        def add_b2(c, first):
+            if first == 0:
+                enc[c] = out_pool.tile([P, BATCH_TILES, W2_CHUNK], F32, name="enc")
+            nc.vector.tensor_tensor(
+                out=enc[c][:, first : first + TILES_PER_BANK, :],
+                in0=enc_acc[(c, first)][:],
+                in1=b2_all[:, chunk_cols(c)].unsqueeze(1).to_broadcast([P, TILES_PER_BANK, W2_CHUNK]),
+                op=ALU.add,
+            )
+            if first + TILES_PER_BANK == BATCH_TILES:
+                nc.sync.dma_start(out=enc_x_rows[:, :, chunk_cols(c)], in_=enc[c][:])
 
-        def turn_pairs(c):
-            w = W2_WIDTHS[c]
-            cols = slice(W2_STARTS[c], W2_STARTS[c + 1])
-            pairs = span(c, c + 1)
+        def multiply_by_cos(c, tiles):
+            n_tiles = tiles.stop - tiles.start
+            pairs = slice(c * CHUNK_PAIRS, (c + 1) * CHUNK_PAIRS)
+            nc.vector.tensor_tensor(
+                out=by_cos[c][:, tiles, :, :],
+                in0=enc[c][:, tiles, :].rearrange("p b (i e) -> p b i e", e=2),
+                in1=cos_amp[:, tiles, pairs].unsqueeze(3).to_broadcast([P, n_tiles, CHUNK_PAIRS, 2]),
+                op=ALU.mult,
+            )
+
+        def multiply_by_sin(c):
+            pairs = slice(c * CHUNK_PAIRS, (c + 1) * CHUNK_PAIRS)
             enc_pairs = enc[c][:].rearrange("p b (i e) -> p b i e", e=2)
-            size = slice(0, BATCH_TILES * w)
-            by_cos = products[:, c % 2, 0, size].rearrange("p (b i e) -> p b i e", b=BATCH_TILES, e=2)
-            def times_cos(tiles):
-                n = tiles.stop - tiles.start
-                nc.vector.tensor_tensor(
-                    out=by_cos[:, tiles, :, :],
-                    in0=enc_pairs[:, tiles, :, :],
-                    in1=cos_amp[:, tiles, pairs].unsqueeze(3).to_broadcast([P, n, w // 2, 2]),
-                    op=ALU.mult,
-                )
-
-            if c < W2_CHUNKS - 1:
-                times_cos(slice(0, BATCH_TILES))
-            by_sin = products[:, c % 2, 1, size].rearrange("p (e b i) -> p e b i", e=2, b=BATCH_TILES)
             nc.vector.scalar_tensor_tensor(
-                out=by_sin[:, 0, :, :],
+                out=by_sin[c][:, 0, :, :],
                 in0=enc_pairs[:, :, :, 1],
                 scalar=-1.0,
                 in1=sin_amp[:, :, pairs],
@@ -432,132 +396,112 @@ def tile_koopmanae_pa_kernel(
                 op1=ALU.mult,
             )
             nc.vector.tensor_tensor(
-                out=by_sin[:, 1, :, :], in0=enc_pairs[:, :, :, 0], in1=sin_amp[:, :, pairs], op=ALU.mult
+                out=by_sin[c][:, 1, :, :], in0=enc_pairs[:, :, :, 0], in1=sin_amp[:, :, pairs], op=ALU.mult
             )
-            if c == W2_CHUNKS - 1:
-                times_cos(slice(0, 2))
-                times_cos(slice(2, 4))
-            turned[c] = (by_cos, by_sin.rearrange("p e b i -> p b i e"))
 
-        def tensor_adds(c):
-            w = W2_WIDTHS[c]
-            by_cos, by_sin_pairs = turned[c]
-            pred[c] = out_pool.tile([P, BATCH_TILES, w // 2, 2], F32, name="pred")
-            tensor_sums = TENSOR_SUMS[c]
-            for lo in range(BATCH_TILES - tensor_sums, BATCH_TILES, 2):
-                rest = slice(lo, min(lo + 2, BATCH_TILES))
-                bank = psum_h.tile([P, rest.stop - lo, w // 2, 2], F32, name="bank", tag="h_acc")
-                nc.tensor.matmul(
-                    out=bank[:], lhsT=ident_f32[:], rhs=by_cos[:, rest, :, :], start=True, stop=False
-                )
-                nc.tensor.matmul(
-                    out=bank[:], lhsT=ident_f32[:], rhs=by_sin_pairs[:, rest, :, :], start=False, stop=True
-                )
-                nc.scalar.copy(out=pred[c][:, rest, :, :], in_=bank[:])
+        def multiply_pairs(c):
+            by_cos[c] = products[:, c % 2, 0, :].rearrange("p (b i e) -> p b i e", b=BATCH_TILES, e=2)
+            by_sin[c] = products[:, c % 2, 1, :].rearrange("p (e b i) -> p e b i", e=2, b=BATCH_TILES)
+            pred[c] = out_pool.tile([P, BATCH_TILES, CHUNK_PAIRS, 2], F32, name="pred")
+            if c < W2_CHUNKS - 1:
+                multiply_by_cos(c, slice(0, BATCH_TILES))
+                multiply_by_sin(c)
+            else:
+                multiply_by_sin(c)
+                multiply_by_cos(c, slice(0, 2))
+                multiply_by_cos(c, slice(2, BATCH_TILES))
 
-        def vector_adds(c):
-            by_cos, by_sin_pairs = turned[c]
-            cols = slice(W2_STARTS[c], W2_STARTS[c + 1])
-            last_chunk = c == W2_CHUNKS - 1
-            for part in (slice(0, 2), slice(2, 4 - TENSOR_SUMS[c])) if last_chunk else (slice(0, BATCH_TILES - TENSOR_SUMS[c]),):
-                if part.stop > part.start: nc.vector.tensor_tensor(
-                    out=pred[c][:, part, :, :],
-                    in0=by_cos[:, part, :, :],
-                    in1=by_sin_pairs[:, part, :, :],
-                    op=ALU.add,
-                )
-                if last_chunk:
-                    nc.sync.dma_start(
-                        out=enc_pred_rows[:, part, cols],
-                        in_=pred[c][:, part, :, :].rearrange("p b i e -> p b (i e)"),
-                    )
-            if not last_chunk:
-                nc.sync.dma_start(
-                    out=enc_pred_rows[:, :, cols], in_=pred[c][:].rearrange("p b i e -> p b (i e)")
-                )
+        def tensor_sums(c):
+            tiles = slice(SUM_TILES_BY_VECTOR, BATCH_TILES)
+            bank = psum_h.tile(
+                [P, BATCH_TILES - SUM_TILES_BY_VECTOR, CHUNK_PAIRS, 2], F32, name="bank", tag="h_acc"
+            )
+            by_sin_pairs = by_sin[c].rearrange("p e b i -> p b i e")
+            nc.tensor.matmul(
+                out=bank[:], lhsT=ident_f32[:], rhs=by_cos[c][:, tiles, :, :], start=True, stop=False
+            )
+            nc.tensor.matmul(
+                out=bank[:], lhsT=ident_f32[:], rhs=by_sin_pairs[:, tiles, :, :], start=False, stop=True
+            )
+            nc.scalar.copy(out=pred[c][:, tiles, :, :], in_=bank[:])
+
+        def vector_sums(c, tiles):
+            by_sin_pairs = by_sin[c].rearrange("p e b i -> p b i e")
+            nc.vector.tensor_tensor(
+                out=pred[c][:, tiles, :, :],
+                in0=by_cos[c][:, tiles, :, :],
+                in1=by_sin_pairs[:, tiles, :, :],
+                op=ALU.add,
+            )
+
+        def store_pred(c, tiles):
+            nc.sync.dma_start(
+                out=enc_pred_rows[:, tiles, chunk_cols(c)],
+                in_=pred[c][:, tiles, :, :].rearrange("p b i e -> p b (i e)"),
+            )
 
         def scalar_works_ahead(k):
-            if k < n_pieces:
-                stage_w1(k)
+            if k < W1_PIECES:
+                scalar_regroups_w1(k)
             else:
-                for job in JOBS[k - n_pieces]:
-                    regroup_w2(job, nc.scalar.copy)
+                regroup_w2(0, k - W1_PIECES, nc.scalar.copy)
 
-        for k in range(n_pieces):
+        for k in range(W1_PIECES):
             c, g = divmod(k, PASSES)
             scalar_works_ahead(k + SCALAR_LEAD)
-            for j in range(len(table_steps)):
-                if TABLE_AT[j] == k:
-                    step, ca, cb = table_steps[j]
-                    step(ca, cb)
-            if X_FIRST:
-                if k < 4:
-                    vector_regroups_w1(k)
-                    quantise_x(k)
-                if 3 <= k < n_pieces - 1:
-                    vector_regroups_w1(k + 1)
-            elif 1 <= k < n_pieces - 1:
+            if k < len(table_steps):
+                step, half = table_steps[k]
+                step(half)
+            if k < PASSES:
+                vector_regroups_w1(k)
+                quantise_x(k)
+            if PASSES - 1 <= k < W1_PIECES - 1:
                 vector_regroups_w1(k + 1)
-            if k + W1_RAW_BUFS < n_pieces:
+            if k + W1_RAW_BUFS < W1_PIECES:
                 load_w1_piece(k + W1_RAW_BUFS)
             quantise_w1(k)
-            if k < PASSES and not X_FIRST:
-                quantise_x(k)
             multiply_w1_piece(k)
             if g == PASSES - 1:
                 tanh_h(c)
             if c > 0 and g == PASSES - 2:
                 if c == 2:
-                    scale_table(sin_amp, 0, HALF)
+                    scale_table(sin_amp, HALF_PAIRS[0])
                 if c == 3:
-                    scale_table(cos_amp, 0, HALF)
+                    scale_table(cos_amp, HALF_PAIRS[0])
                 regroup_h(c - 1)
             if c > 0 and g == PASSES - 1:
                 quantise_h(c - 1)
 
-        def prepare(c):
-            if c >= TAIL_FROM:
-                for step in (take_abs, take_sin, take_cos):
-                    step(c, c + 1)
-            for g in range(PASSES):
-                regroup_w2(c * PASSES + g, nc.scalar.copy)
-
-        products = keep.tile([P, 2, 2, BATCH_TILES * 256], F32, align_bytes=64, name="products", tag="x_then_products")
+        products = keep.tile(
+            [P, 2, 2, BATCH_TILES * W2_CHUNK], F32, align_bytes=64, name="products", tag="x_then_products"
+        )
         last = W1_CHUNKS - 1
-        if not JOB3_V:
-            for job in range(sum(len(j) for j in JOBS), PASSES):
-                regroup_w2(job, nc.scalar.copy)
-        quantise_w2(0, (0,))
-        scale_table(sin_amp, HALF, TAIL_FROM)
-        if EARLY4:
-            scale_table(cos_amp, HALF, TAIL_FROM)
-        if JOB3_V:
-            for job in range(sum(len(j) for j in JOBS), PASSES):
-                regroup_w2(job, nc.vector.tensor_copy)
-        regroup_h(last, H_SPLIT)
-        quantise_w2(0, (2,))
+        quantise_w2(0, 0)
+        scale_table(sin_amp, HALF_PAIRS[1])
+        regroup_w2(0, PASSES - 1, nc.vector.tensor_copy)
+        regroup_h(last)
+        quantise_w2(0, 2)
         quantise_h(last)
-        prepare(1)
+        scalar_regroups_w2_chunk(1)
         multiply_w2_chunk(0)
-        if not EARLY4:
-            scale_table(cos_amp, HALF, TAIL_FROM)
+        scale_table(cos_amp, HALF_PAIRS[1])
 
         for c in range(W2_CHUNKS):
-            def between():
-                if c + 1 < W2_CHUNKS:
-                    quantise_w2(c + 1, (0,))
-
-            add_b2(c, between)
-            if c > 0:
-                vector_adds(c - 1)
-            if c + 2 < W2_CHUNKS:
-                prepare(c + 2)
+            add_b2(c, 0)
             if c + 1 < W2_CHUNKS:
-                quantise_w2(c + 1, (2,) if INTER else None)
+                quantise_w2(c + 1, 0)
+            add_b2(c, TILES_PER_BANK)
+            if c > 0:
+                vector_sums(c - 1, slice(0, SUM_TILES_BY_VECTOR))
+                store_pred(c - 1, slice(0, BATCH_TILES))
+            if c + 2 < W2_CHUNKS:
+                scalar_regroups_w2_chunk(c + 2)
+            if c + 1 < W2_CHUNKS:
+                quantise_w2(c + 1, 2)
                 multiply_w2_chunk(c + 1)
-            if c >= TAIL_FROM:
-                scale_table(sin_amp, c, c + 1)
-                scale_table(cos_amp, c, c + 1)
-            turn_pairs(c)
-            tensor_adds(c)
-        vector_adds(W2_CHUNKS - 1)
+            multiply_pairs(c)
+            if c + 1 < W2_CHUNKS:
+                tensor_sums(c)
+        for tiles in (slice(0, 2), slice(2, BATCH_TILES)):
+            vector_sums(W2_CHUNKS - 1, tiles)
+            store_pred(W2_CHUNKS - 1, tiles)

import math
from contextlib import ExitStack

import concourse.mybir as mybir
from concourse.masks import make_identity

F32 = mybir.dt.float32
BF16 = mybir.dt.bfloat16
U32 = mybir.dt.uint32
I32 = mybir.dt.int32
U8 = mybir.dt.uint8
FP8X4 = mybir.dt.float8_e4m3fn_x4
ALU = mybir.AluOpType
ACT = mybir.ActivationFunctionType

P = 128
PACK = 4
K_PASS = P * PACK

BATCH, D_IN, HID, PAIRS = 512, 2048, 2048, 512
LATENT = 2 * PAIRS
BATCH_TILES = BATCH // P
PASSES = D_IN // K_PASS
HID_TILES = HID // P

W1_CHUNK = K_PASS
W1_CHUNKS = HID // W1_CHUNK
W1_PIECES = W1_CHUNKS * PASSES
W2_CHUNK = 256
W2_CHUNKS = LATENT // W2_CHUNK
CHUNK_PAIRS = W2_CHUNK // 2
TILES_PER_BANK = 2
QUANT_PASSES = 2

W1_VECTOR_COLS = 288
SCALAR_LEAD = 3
W1_RAW_BUFS = 7
X_TILES_BY_SCALAR = BATCH_TILES - 1
SUM_TILES_BY_VECTOR = 2
RUN = 8
HALF_PAIRS = (slice(0, PAIRS // 2), slice(PAIRS // 2, PAIRS))

FLOPS = 2 * BATCH * D_IN * HID + 2 * BATCH * HID * LATENT


def regroup(copy, grouped, planes):
    copy(
        out=grouped.rearrange("p (c i) t -> p c t i", i=RUN),
        in_=planes.rearrange("p t (c i) -> p c t i", i=RUN),
    )


def tile_koopmanae_pa_kernel(
    tc, x, delta_t, W_enc1, b_enc1, W_enc2, b_enc2, amplitudes, frequencies, out_0, out_1
):
    nc = tc.nc
    with ExitStack() as ctx:
        ctx.enter_context(tc.manual_schedule())
        keep = ctx.enter_context(tc.tile_pool(name="keep", bufs=1))
        w1_raw_pool = ctx.enter_context(tc.tile_pool(name="w1_raw", bufs=W1_RAW_BUFS))
        w1_grouped_pool = ctx.enter_context(tc.tile_pool(name="w1_grouped", bufs=SCALAR_LEAD + 2))
        grouped_pool = ctx.enter_context(tc.tile_pool(name="grouped", bufs=5))
        w1_mx_pool = ctx.enter_context(tc.tile_pool(name="w1_mx", bufs=2))
        psum_h = ctx.enter_context(tc.psum_pool(name="psum_h", bufs=6))
        psum_stage = ctx.enter_context(tc.psum_pool(name="psum_stage", bufs=1))

        x_codes = keep.tile([P, PASSES, BATCH], U32, align_bytes=64)
        x_scales = keep.tile([P, PASSES, BATCH], U8, align_bytes=64)
        h_codes = keep.tile([P, PASSES, BATCH], U32, align_bytes=64)
        h_scales = keep.tile([P, PASSES, BATCH], U8, align_bytes=64)
        w2_codes = keep.tile([P, LATENT * PASSES], U32, align_bytes=64)
        w2_scales = keep.tile([P, LATENT * PASSES], U8, align_bytes=64)

        ident_bf16 = keep.tile([P, P], BF16)
        make_identity(nc, ident_bf16[:])
        ident_f32 = keep.tile([P, P], F32)
        make_identity(nc, ident_f32[:])

        rows = keep.tile([P, P], BF16)
        nc.vector.memset(rows[:], 0.0)
        nc.sync.dma_start(out=rows[0:HID_TILES, :], in_=b_enc1.rearrange("(m p) -> m p", p=P))
        nc.sync.dma_start(
            out=rows[HID_TILES : HID_TILES + BATCH_TILES, :],
            in_=delta_t.rearrange("(b p) -> b p", p=P),
        )
        FREQ_ROW, AMPL_ROW = 0, 1
        vectors = keep.tile([P, PAIRS], BF16)
        nc.vector.memset(vectors[:], 0.0)
        nc.sync.dma_start(
            out=vectors[FREQ_ROW : FREQ_ROW + 1, :], in_=frequencies.rearrange("(r n) -> r n", r=1)
        )
        nc.sync.dma_start(
            out=vectors[AMPL_ROW : AMPL_ROW + 1, :], in_=amplitudes.rearrange("(r n) -> r n", r=1)
        )
        b2_all = keep.tile([P, LATENT], BF16)

        def spread_row(r):
            bank = psum_h.tile([P, PAIRS], F32, name="spread", tag="h_acc")
            nc.tensor.matmul(
                out=bank[:],
                lhsT=ident_bf16[:, r : r + 1].to_broadcast([P, P]),
                rhs=vectors[:],
                start=True,
                stop=True,
            )
            return bank

        w1_rows = W_enc1.rearrange("(g p j) n -> g p j n", p=P, j=PACK)
        w2_rows = W_enc2.rearrange("(g t p) n -> g p t n", t=PACK, p=P)
        w2_raw = keep.tile([P, PASSES, PACK, LATENT], BF16)
        w1_raw = {}

        def load_w1_piece(k):
            c, g = divmod(k, PASSES)
            w1_raw[k] = w1_raw_pool.tile([P, PACK, W1_CHUNK], BF16, name="w1_raw")
            nc.sync.dma_start(
                out=w1_raw[k][:], in_=w1_rows[g, :, :, c * W1_CHUNK : (c + 1) * W1_CHUNK]
            )
            if k == W1_PIECES - 1:
                for w2_pass in range(PASSES):
                    nc.sync.dma_start(out=w2_raw[:, w2_pass, :, :], in_=w2_rows[w2_pass])
                nc.sync.dma_start(out=b2_all[:], in_=b_enc2.partition_broadcast(P))

        w1_grouped = {}
        w1_mx = {}
        h_acc = {}
        h_planes = {}
        h_grouped = {}

        def vector_cols(k):
            return W1_CHUNK if k < PASSES else W1_VECTOR_COLS

        def scalar_regroups_w1(k):
            w1_grouped[k] = w1_grouped_pool.tile(
                [P, W1_CHUNK, PACK], BF16, align_bytes=64, name="w1_grouped"
            )
            if vector_cols(k) < W1_CHUNK:
                cols = slice(vector_cols(k), W1_CHUNK)
                regroup(nc.scalar.copy, w1_grouped[k][:, cols, :], w1_raw[k][:, :, cols])

        def vector_regroups_w1(k):
            cols = slice(0, vector_cols(k))
            regroup(nc.vector.tensor_copy, w1_grouped[k][:, cols, :], w1_raw[k][:, :, cols])

        def quantise_x(g):
            nc.vector.quantize_mx(
                out=x_codes[:, g, :].bitcast(FP8X4),
                scales=x_scales[:, g, :],
                in_=x_grouped[:, g, :, :].rearrange("p b t -> p (b t)"),
            )

        def quantise_w1(k):
            c, g = divmod(k, PASSES)
            if g == 0:
                w1_mx[c] = (
                    w1_mx_pool.tile([P, PASSES, W1_CHUNK], U32, align_bytes=64, name="w1_codes"),
                    w1_mx_pool.tile([P, PASSES, W1_CHUNK], U8, align_bytes=64, name="w1_scales"),
                )
            codes, scales = w1_mx[c]
            nc.vector.quantize_mx(
                out=codes[:, g, :].bitcast(FP8X4),
                scales=scales[:, g, :],
                in_=w1_grouped[k][:].rearrange("p n t -> p (n t)"),
            )

        def multiply_w1_piece(k):
            c, g = divmod(k, PASSES)
            if g == 0:
                h_acc[c] = [psum_h.tile([P, BATCH], F32, name="h_acc") for t in range(PACK)]
            codes, scales = w1_mx[c]
            for t in range(PACK):
                units = slice(t * P, (t + 1) * P)
                nc.tensor.matmul_mx(
                    out=h_acc[c][t][:],
                    lhsT=codes[:, g, units].bitcast(FP8X4),
                    lhsT_scale=scales[:, g, units],
                    rhs=x_codes[:, g, :].bitcast(FP8X4),
                    rhs_scale=x_scales[:, g, :],
                    start=(g == 0),
                    stop=(g == PASSES - 1),
                )

        def tanh_h(c):
            h_planes[c] = h_pool.tile([P, PACK, BATCH], BF16, name="h_planes")
            for t in range(PACK):
                m = c * PACK + t
                nc.scalar.activation(
                    out=h_planes[c][:, t, :], in_=h_acc[c][t][:], func=ACT.Tanh, bias=b1_col[:, m : m + 1]
                )

        def regroup_h(c):
            h_grouped[c] = grouped_pool.tile(
                [P, BATCH, PACK], BF16, align_bytes=64, name="h_grouped", tag="grouped"
            )
            regroup(nc.vector.tensor_copy, h_grouped[c][:], h_planes[c][:])

        def quantise_h(c):
            nc.vector.quantize_mx(
                out=h_codes[:, c, :].bitcast(FP8X4),
                scales=h_scales[:, c, :],
                in_=h_grouped[c][:].rearrange("p b t -> p (b t)"),
            )

        with tc.tile_pool(name="early", bufs=1) as early:
            x_sb = early.tile([P, BATCH_TILES, D_IN], BF16)
            for b in range(BATCH_TILES):
                nc.sync.dma_start(out=x_sb[:, b, :], in_=x[b * P : (b + 1) * P, :])
            for k in range(W1_RAW_BUFS):
                load_w1_piece(k)

            columns_ps = psum_stage.tile([P, P], BF16, name="columns_ps", tag="stage")
            nc.tensor.transpose(columns_ps[:], rows[:], ident_bf16[:])
            columns = keep.tile([P, HID_TILES + BATCH_TILES], F32)
            nc.vector.tensor_copy(out=columns[:], in_=columns_ps[:, 0 : HID_TILES + BATCH_TILES])
            b1_col = columns[:, 0:HID_TILES]
            dt_col = columns[:, HID_TILES : HID_TILES + BATCH_TILES]

            dt_turns = keep.tile([P, BATCH_TILES], F32)
            nc.vector.tensor_scalar(
                out=dt_turns[:], in0=dt_col, scalar1=1.0 / (2.0 * math.pi), scalar2=None, op0=ALU.mult
            )
            freq_all = early.tile([P, PAIRS], BF16)
            nc.vector.tensor_copy(out=freq_all[:], in_=spread_row(FREQ_ROW)[:])
            ln_ampl = early.tile([P, PAIRS], F32)
            nc.scalar.activation(out=ln_ampl[:], in_=spread_row(AMPL_ROW)[:], func=ACT.Ln)

            whole = early.tile([P, BATCH_TILES, PAIRS], I32)
            sin_amp = keep.tile([P, BATCH_TILES, PAIRS], F32)
            cos_amp = keep.tile([P, BATCH_TILES, PAIRS], F32)
            power = keep.tile([P, BATCH_TILES, PAIRS], F32)
            for b in range(BATCH_TILES):
                nc.vector.tensor_scalar(
                    out=whole[:, b, :],
                    in0=freq_all[:],
                    scalar1=dt_turns[:, b : b + 1],
                    scalar2=None,
                    op0=ALU.mult,
                )
            for b in range(BATCH_TILES):
                nc.vector.scalar_tensor_tensor(
                    out=sin_amp[:, b, :],
                    in0=freq_all[:],
                    scalar=dt_turns[:, b : b + 1],
                    in1=whole[:, b, :],
                    op0=ALU.mult,
                    op1=ALU.subtract,
                )

            def take_power(b):
                nc.scalar.activation(
                    out=power[:, b, :], in_=ln_ampl[:], func=ACT.Exp, scale=dt_col[:, b : b + 1]
                )

            x_grouped = keep.tile(
                [P, PASSES, BATCH, PACK], BF16, align_bytes=64, name="x_grouped", tag="x_then_products"
            )
            x_grouped_words = (
                x_grouped[:]
                .rearrange("p g b t -> p (g b t)")
                .bitcast(F32)
                .rearrange("p (g b u) -> p g b u", g=PASSES, u=2)
            )
            for k in range(SCALAR_LEAD):
                scalar_regroups_w1(k)
            take_power(0)
            for b in range(BATCH_TILES):
                words = x_sb[:, b, :].bitcast(F32).rearrange("p (g q u) -> p g u q", g=PASSES, u=2)
                for half in range(2):
                    xt = psum_h.tile([P, 2, 2, P], F32, name="xt", tag="h_acc")
                    for j in range(2):
                        for u in range(2):
                            nc.tensor.transpose(
                                xt[:, j, u, :], words[:, 2 * half + j, u, :], ident_f32[:]
                            )
                    copy = nc.scalar.copy if b < X_TILES_BY_SCALAR else nc.vector.tensor_copy
                    copy(
                        out=x_grouped_words[:, 2 * half : 2 * half + 2, b * P : (b + 1) * P, :],
                        in_=xt[:].rearrange("p j u b -> p j b u"),
                    )
                if b < BATCH_TILES - 1:
                    take_power(b + 1)

            set_loader = keep.tile([P, 1], F32)
            nc.scalar.activation(out=set_loader[:], in_=ident_f32[:, 0:1], func=ACT.Silu)

        def take_abs(half):
            nc.scalar.activation(out=cos_amp[:, :, half], in_=sin_amp[:, :, half], func=ACT.Abs)

        def take_sin(half):
            nc.scalar.activation(
                out=sin_amp[:, :, half], in_=sin_amp[:, :, half], func=ACT.Sin, scale=2.0 * math.pi
            )

        def take_cos(half):
            nc.scalar.activation(
                out=cos_amp[:, :, half],
                in_=cos_amp[:, :, half],
                func=ACT.Sin,
                scale=-2.0 * math.pi,
                bias=math.pi / 2.0,
            )

        def scale_table(table, half):
            nc.vector.tensor_tensor(
                out=table[:, :, half], in0=table[:, :, half], in1=power[:, :, half], op=ALU.mult
            )

        table_steps = [(step, half) for half in HALF_PAIRS for step in (take_abs, take_sin, take_cos)]

        h_pool = ctx.enter_context(tc.tile_pool(name="h", bufs=2))
        out_pool = ctx.enter_context(tc.tile_pool(name="out", bufs=2))

        w2_grouped = {}
        enc_acc = {}
        enc = {}
        by_cos = {}
        by_sin = {}
        pred = {}
        enc_x_rows = out_1.rearrange("(b p) n -> p b n", p=P)
        enc_pred_rows = out_0.rearrange("(b p) n -> p b n", p=P)

        def chunk_cols(c):
            return slice(c * W2_CHUNK, (c + 1) * W2_CHUNK)

        def regroup_w2(c, g, copy):
            first = g - g % QUANT_PASSES
            if g == first:
                w2_grouped[(c, first)] = grouped_pool.tile(
                    [P, QUANT_PASSES, W2_CHUNK, PACK], BF16, align_bytes=64, name="w2_grouped", tag="grouped"
                )
            regroup(copy, w2_grouped[(c, first)][:, g - first, :, :], w2_raw[:, g, :, chunk_cols(c)])

        def scalar_regroups_w2_chunk(c):
            for g in range(PASSES):
                regroup_w2(c, g, nc.scalar.copy)

        def quantise_w2(c, first):
            start = (c * PASSES + first) * W2_CHUNK
            words = slice(start, start + QUANT_PASSES * W2_CHUNK)
            nc.vector.quantize_mx(
                out=w2_codes[:, words].bitcast(FP8X4),
                scales=w2_scales[:, words],
                in_=w2_grouped[(c, first)][:].rearrange("p g n t -> p (g n t)"),
            )

        def multiply_w2_chunk(c):
            for first in range(0, BATCH_TILES, TILES_PER_BANK):
                acc = psum_h.tile([P, TILES_PER_BANK, W2_CHUNK], F32, name="enc_acc", tag="h_acc")
                enc_acc[(c, first)] = acc
                for j in range(TILES_PER_BANK):
                    batch = slice((first + j) * P, (first + j + 1) * P)
                    for g in range(PASSES):
                        start = (c * PASSES + g) * W2_CHUNK
                        words = slice(start, start + W2_CHUNK)
                        nc.tensor.matmul_mx(
                            out=acc[:, j, :],
                            lhsT=h_codes[:, g, batch].bitcast(FP8X4),
                            lhsT_scale=h_scales[:, g, batch],
                            rhs=w2_codes[:, words].bitcast(FP8X4),
                            rhs_scale=w2_scales[:, words],
                            start=(g == 0),
                            stop=(g == PASSES - 1),
                        )

        def add_b2(c, first):
            if first == 0:
                enc[c] = out_pool.tile([P, BATCH_TILES, W2_CHUNK], F32, name="enc")
            nc.vector.tensor_tensor(
                out=enc[c][:, first : first + TILES_PER_BANK, :],
                in0=enc_acc[(c, first)][:],
                in1=b2_all[:, chunk_cols(c)].unsqueeze(1).to_broadcast([P, TILES_PER_BANK, W2_CHUNK]),
                op=ALU.add,
            )
            if first + TILES_PER_BANK == BATCH_TILES:
                nc.sync.dma_start(out=enc_x_rows[:, :, chunk_cols(c)], in_=enc[c][:])

        def multiply_by_cos(c, tiles):
            n_tiles = tiles.stop - tiles.start
            pairs = slice(c * CHUNK_PAIRS, (c + 1) * CHUNK_PAIRS)
            nc.vector.tensor_tensor(
                out=by_cos[c][:, tiles, :, :],
                in0=enc[c][:, tiles, :].rearrange("p b (i e) -> p b i e", e=2),
                in1=cos_amp[:, tiles, pairs].unsqueeze(3).to_broadcast([P, n_tiles, CHUNK_PAIRS, 2]),
                op=ALU.mult,
            )

        def multiply_by_sin(c):
            pairs = slice(c * CHUNK_PAIRS, (c + 1) * CHUNK_PAIRS)
            enc_pairs = enc[c][:].rearrange("p b (i e) -> p b i e", e=2)
            nc.vector.scalar_tensor_tensor(
                out=by_sin[c][:, 0, :, :],
                in0=enc_pairs[:, :, :, 1],
                scalar=-1.0,
                in1=sin_amp[:, :, pairs],
                op0=ALU.mult,
                op1=ALU.mult,
            )
            nc.vector.tensor_tensor(
                out=by_sin[c][:, 1, :, :], in0=enc_pairs[:, :, :, 0], in1=sin_amp[:, :, pairs], op=ALU.mult
            )

        def multiply_pairs(c):
            by_cos[c] = products[:, c % 2, 0, :].rearrange("p (b i e) -> p b i e", b=BATCH_TILES, e=2)
            by_sin[c] = products[:, c % 2, 1, :].rearrange("p (e b i) -> p e b i", e=2, b=BATCH_TILES)
            pred[c] = out_pool.tile([P, BATCH_TILES, CHUNK_PAIRS, 2], F32, name="pred")
            if c < W2_CHUNKS - 1:
                multiply_by_cos(c, slice(0, BATCH_TILES))
                multiply_by_sin(c)
            else:
                multiply_by_sin(c)
                multiply_by_cos(c, slice(0, 2))
                multiply_by_cos(c, slice(2, BATCH_TILES))

        def tensor_sums(c):
            tiles = slice(SUM_TILES_BY_VECTOR, BATCH_TILES)
            bank = psum_h.tile(
                [P, BATCH_TILES - SUM_TILES_BY_VECTOR, CHUNK_PAIRS, 2], F32, name="bank", tag="h_acc"
            )
            by_sin_pairs = by_sin[c].rearrange("p e b i -> p b i e")
            nc.tensor.matmul(
                out=bank[:], lhsT=ident_f32[:], rhs=by_cos[c][:, tiles, :, :], start=True, stop=False
            )
            nc.tensor.matmul(
                out=bank[:], lhsT=ident_f32[:], rhs=by_sin_pairs[:, tiles, :, :], start=False, stop=True
            )
            nc.scalar.copy(out=pred[c][:, tiles, :, :], in_=bank[:])

        def vector_sums(c, tiles):
            by_sin_pairs = by_sin[c].rearrange("p e b i -> p b i e")
            nc.vector.tensor_tensor(
                out=pred[c][:, tiles, :, :],
                in0=by_cos[c][:, tiles, :, :],
                in1=by_sin_pairs[:, tiles, :, :],
                op=ALU.add,
            )

        def store_pred(c, tiles):
            nc.sync.dma_start(
                out=enc_pred_rows[:, tiles, chunk_cols(c)],
                in_=pred[c][:, tiles, :, :].rearrange("p b i e -> p b (i e)"),
            )

        def scalar_works_ahead(k):
            if k < W1_PIECES:
                scalar_regroups_w1(k)
            else:
                regroup_w2(0, k - W1_PIECES, nc.scalar.copy)

        for k in range(W1_PIECES):
            c, g = divmod(k, PASSES)
            scalar_works_ahead(k + SCALAR_LEAD)
            if k < len(table_steps):
                step, half = table_steps[k]
                step(half)
            if k < PASSES:
                vector_regroups_w1(k)
                quantise_x(k)
            if PASSES - 1 <= k < W1_PIECES - 1:
                vector_regroups_w1(k + 1)
            if k + W1_RAW_BUFS < W1_PIECES:
                load_w1_piece(k + W1_RAW_BUFS)
            quantise_w1(k)
            multiply_w1_piece(k)
            if g == PASSES - 1:
                tanh_h(c)
            if c > 0 and g == PASSES - 2:
                if c == 2:
                    scale_table(sin_amp, HALF_PAIRS[0])
                if c == 3:
                    scale_table(cos_amp, HALF_PAIRS[0])
                regroup_h(c - 1)
            if c > 0 and g == PASSES - 1:
                quantise_h(c - 1)

        products = keep.tile(
            [P, 2, 2, BATCH_TILES * W2_CHUNK], F32, align_bytes=64, name="products", tag="x_then_products"
        )
        last = W1_CHUNKS - 1
        quantise_w2(0, 0)
        scale_table(sin_amp, HALF_PAIRS[1])
        regroup_w2(0, PASSES - 1, nc.vector.tensor_copy)
        regroup_h(last)
        quantise_w2(0, 2)
        quantise_h(last)
        scalar_regroups_w2_chunk(1)
        multiply_w2_chunk(0)
        scale_table(cos_amp, HALF_PAIRS[1])

        for c in range(W2_CHUNKS):
            add_b2(c, 0)
            if c + 1 < W2_CHUNKS:
                quantise_w2(c + 1, 0)
            add_b2(c, TILES_PER_BANK)
            if c > 0:
                vector_sums(c - 1, slice(0, SUM_TILES_BY_VECTOR))
                store_pred(c - 1, slice(0, BATCH_TILES))
            if c + 2 < W2_CHUNKS:
                scalar_regroups_w2_chunk(c + 2)
            if c + 1 < W2_CHUNKS:
                quantise_w2(c + 1, 2)
                multiply_w2_chunk(c + 1)
            multiply_pairs(c)
            if c + 1 < W2_CHUNKS:
                tensor_sums(c)
        for tiles in (slice(0, 2), slice(2, BATCH_TILES)):
            vector_sums(W2_CHUNKS - 1, tiles)
            store_pred(W2_CHUNKS - 1, tiles)
